import numpy as np
import ml_dtypes


def mxq(x, axis, fmt="e4m3"):
    dtype, down = {"e4m3": (ml_dtypes.float8_e4m3fn, 7), "e5m2": (ml_dtypes.float8_e5m2, 14)}[fmt]
    v = np.moveaxis(np.asarray(x, np.float32).astype(ml_dtypes.bfloat16).astype(np.float64), axis, -1)
    blocks = v.reshape(v.shape[:-1] + (-1, 32))
    amax = np.abs(blocks).max(-1, keepdims=True)
    byte = np.maximum(np.where(amax > 0, np.frexp(amax)[1] - 1 + 127, 0) - down, 1)
    scale = np.exp2(byte - 127.0)
    codes = (blocks / scale).astype(np.float32).astype(dtype).astype(np.float64)
    return np.moveaxis((codes * scale).reshape(v.shape), -1, axis)


WIDE = False


def mx_kscale(k):
    if not WIDE:
        return np.ones(k)
    levels = np.array([10, -10, 5, -5, 0])
    a = np.random.permutation(np.resize(levels, k // 512 * 4)).reshape(k // 512, 4)
    idx = np.arange(k)
    return np.exp2(a[idx // 512, idx % 128 // 32])


BF16 = ml_dtypes.bfloat16


def bf(x):
    return np.asarray(x, np.float32).astype(BF16)


def f64(x):
    return np.asarray(x).astype(np.float64)


B, C, H, W, NH = 4, 512, 32, 32, 4
N = H * W
DH = C // NH
BN_EPS = 1e-5


def signed_gain(n):
    return np.sign(np.random.standard_normal(n)) * (0.6 + 0.8 * np.random.random(n))


def conv_bn(x, w, b, g, beta):
    y = (mxq(f64(w), 1, "e4m3") @ mxq(f64(x).reshape(B, C, N), 1, "e4m3")) + f64(b)[None, :, None]
    return y * (f64(g) / np.sqrt(1.0 + BN_EPS))[None, :, None] + f64(beta)[None, :, None]


def l2norm(t):
    return t / np.maximum(np.sqrt(np.sum(t * t, axis=-1, keepdims=True)), 1e-12)


def setup_inputs():
    s = mx_kscale(C)
    return {"x1": bf(np.random.standard_normal((B, C, H, W)) * s[None, :, None, None]),
            "x2": bf(np.random.standard_normal((B, C, H, W)) * s[None, :, None, None]),
            "k_w": bf(np.random.standard_normal((C, C)) / np.sqrt(C) / s[None, :]),
            "k_b": bf(np.random.standard_normal(C) * 0.15),
            "q_w": bf(np.random.standard_normal((C, C)) / np.sqrt(C) / s[None, :]),
            "q_b": bf(np.random.standard_normal(C) * 0.15),
            "temperature": bf(np.sqrt(N) * (1.0 + 0.2 * np.random.standard_normal((NH, 1, 1)))),
            "bnk_w": bf(signed_gain(C)),
            "bnk_b": bf(np.random.standard_normal(C) * 0.15),
            "bnq_w": bf(signed_gain(C)),
            "bnq_b": bf(np.random.standard_normal(C) * 0.15)}


def reference(x1, x2, k_w, k_b, q_w, q_b, temperature, bnk_w, bnk_b, bnq_w, bnq_b):
    k = l2norm(conv_bn(x1, k_w, k_b, bnk_w, bnk_b).reshape(B, NH, DH, N))
    q = l2norm(conv_bn(x2, q_w, q_b, bnq_w, bnq_b).reshape(B, NH, DH, N))
    return (mxq(q, 3, "e4m3") @ mxq(k, 3, "e4m3").transpose(0, 1, 3, 2)) * f64(temperature)[None]

@@ -1,0 +1,357 @@
+import math
+from contextlib import ExitStack
+
+import concourse.mybir as mybir
+from concourse.masks import make_identity
+
+F32 = mybir.dt.float32
+BF16 = mybir.dt.bfloat16
+U32 = mybir.dt.uint32
+U8 = mybir.dt.uint8
+FP8X4 = mybir.dt.float8_e4m3fn_x4
+ACT = mybir.ActivationFunctionType
+ALU = mybir.AluOpType
+
+P = 128
+PACK = 4
+BATCH = 4
+CHANNELS = 512
+PIXELS = 1024
+HEADS = 4
+SIDES = 2
+BANK = 512
+HALVES = PIXELS // BANK
+PASSES = PIXELS // (P * PACK)
+SLABS = BATCH * SIDES
+UNITS = SLABS * HEADS
+CHUNK = 256
+CHUNKS_PER_SLAB = PIXELS // CHUNK
+CHUNKS = SLABS * CHUNKS_PER_SLAB
+BN_EPS = 1e-5
+INV_STD = 1.0 / math.sqrt(1.0 + BN_EPS)
+MAX_INV_NORM = 1e12
+
+FLOPS = 2 * SLABS * CHANNELS * CHANNELS * PIXELS + 2 * BATCH * HEADS * P * P * PIXELS
+
+
+def tile_transposedattention_fusion_pa_t_kernel(
+    tc, x1, x2, k_w, k_b, q_w, q_b, temperature, bnk_w, bnk_b, bnq_w, bnq_b, out
+):
+    nc = tc.nc
+    with ExitStack() as ctx:
+        ctx.enter_context(tc.manual_schedule())
+        const = ctx.enter_context(tc.tile_pool(name="const", bufs=1))
+        x_pool = ctx.enter_context(tc.tile_pool(name="x_pool", bufs=3))
+        unit_pool = ctx.enter_context(tc.tile_pool(name="unit_pool", bufs=3))
+        code_pool = ctx.enter_context(tc.tile_pool(name="code_pool", bufs=8))
+        small = ctx.enter_context(tc.tile_pool(name="small", bufs=4))
+        psum_y = ctx.enter_context(tc.psum_pool(name="psum_y", bufs=5))
+        psum_turned = ctx.enter_context(tc.psum_pool(name="psum_turned", bufs=2))
+        psum_scores = ctx.enter_context(tc.psum_pool(name="psum_scores", bufs=1))
+
+        vec_rows = const.tile([P, P], BF16, name="vec_rows")
+        nc.vector.memset(vec_rows[:], 0.0)
+        one = const.tile([P, 1], F32, name="one")
+        nc.vector.memset(one[:], 1.0)
+        for v, vec in enumerate((k_b, bnk_w, bnk_b, q_b, bnq_w, bnq_b)):
+            nc.scalar.dma_start(
+                out=vec_rows[HEADS * v : HEADS * (v + 1), :], in_=vec.rearrange("(h o) -> h o", o=P)
+            )
+        temp_bf16 = const.tile([P, HEADS], BF16, name="temp_bf16")
+        nc.scalar.dma_start(
+            out=temp_bf16[:], in_=temperature.rearrange("h a b -> (h a b)").partition_broadcast(P)
+        )
+
+        w_rows = {}
+        x_rows = {}
+
+        def load_weight(side, w):
+            w_rows[side] = const.tile([P, HEADS * CHANNELS], BF16, name="w_rows%d" % side)
+            nc.sync.dma_start(
+                out=w_rows[side][:].rearrange("o (h c) -> o h c", h=HEADS),
+                in_=w.rearrange("(h o) c -> o h c", o=P),
+            )
+
+        def load_slab(slab, x):
+            x_rows[slab] = const.tile([P, PACK, PIXELS], BF16, name="x_rows%d" % slab)
+            nc.sync.dma_start(
+                out=x_rows[slab][:],
+                in_=x[slab // SIDES].rearrange("(p j) h w -> p j (h w)", j=PACK),
+            )
+
+        load_weight(0, k_w)
+        load_slab(0, x1)
+        load_weight(1, q_w)
+        load_slab(1, x2)
+        for b in range(1, BATCH):
+            load_slab(SIDES * b, x1)
+            load_slab(SIDES * b + 1, x2)
+
+        warm = const.tile([P, 1], F32, name="warm")
+        nc.scalar.activation(out=warm[:], in_=one[:], func=ACT.Abs_reciprocal_sqrt)
+
+        ident = const.tile([P, P], F32, name="ident")
+        make_identity(nc, ident[:])
+
+        vec_rows_f32 = const.tile([P, P], F32, name="vec_rows_f32")
+        nc.vector.tensor_copy(out=vec_rows_f32[:], in_=vec_rows[:])
+        vec_turned = psum_scores.tile([P, P], F32, tag="scores", name="vec_turned")
+        nc.tensor.transpose(vec_turned[:], vec_rows_f32[:], ident[:])
+        vec_cols = const.tile([P, SIDES, 3, HEADS], F32, name="vec_cols")
+        nc.vector.tensor_copy(
+            out=vec_cols[:].rearrange("o s v h -> o (s v h)"), in_=vec_turned[:, 0 : SIDES * 3 * HEADS]
+        )
+        affine = const.tile([P, SIDES, HEADS, 2], F32, name="affine")
+        nc.vector.tensor_scalar(
+            out=affine[:, :, :, 0], in0=vec_cols[:, :, 1, :], scalar1=INV_STD, scalar2=None, op0=ALU.mult
+        )
+        nc.vector.tensor_tensor(
+            out=affine[:, :, :, 1], in0=vec_cols[:, :, 0, :], in1=affine[:, :, :, 0], op=ALU.mult
+        )
+        nc.vector.tensor_tensor(
+            out=affine[:, :, :, 1], in0=affine[:, :, :, 1], in1=vec_cols[:, :, 2, :], op=ALU.add
+        )
+        temp = const.tile([P, HEADS], F32, name="temp")
+        nc.vector.tensor_copy(out=temp[:], in_=temp_bf16[:])
+
+        w_grouped = {}
+        w_codes = {}
+        w_scales = {}
+
+        def turn_weight(side):
+            words = w_rows[side][:].bitcast(F32).rearrange("o (h p u) -> o h u p", h=HEADS, u=2)
+            w_grouped[side] = const.tile(
+                [P, HEADS * P * PACK], BF16, name="w_grouped%d" % side, align_bytes=64
+            )
+            grouped_words = w_grouped[side][:].bitcast(F32).rearrange("p (h o u) -> p h o u", h=HEADS, u=2)
+            for pair in range(HEADS // 2):
+                turned = psum_turned.tile([P, 2, 2, P], F32, tag="turned", name="w_turned")
+                for i in range(2):
+                    for u in range(2):
+                        nc.tensor.transpose(turned[:, i, u, :], words[:, 2 * pair + i, u, :], ident[:])
+                nc.scalar.copy(
+                    out=grouped_words[:, 2 * pair : 2 * pair + 2, :, :],
+                    in_=turned[:].rearrange("p i u o -> p i o u"),
+                )
+
+        def quantise_weight(side):
+            w_codes[side] = const.tile([P, CHANNELS], U32, name="w_codes%d" % side, align_bytes=64)
+            w_scales[side] = const.tile([P, CHANNELS], U8, name="w_scales%d" % side, align_bytes=64)
+            nc.vector.quantize_mx(
+                out=w_codes[side][:].bitcast(FP8X4), scales=w_scales[side][:], in_=w_grouped[side][:]
+            )
+
+        x_grouped = {}
+        x_codes = {}
+        x_scales = {}
+
+        def regroup_x(chunk):
+            if not 0 <= chunk < CHUNKS:
+                return
+            slab, c = divmod(chunk, CHUNKS_PER_SLAB)
+            if c == 0:
+                x_grouped[slab] = x_pool.tile(
+                    [P, PIXELS, PACK], BF16, tag="x_grouped", name="x_grouped", align_bytes=64
+                )
+            cols = slice(c * CHUNK, (c + 1) * CHUNK)
+            nc.vector.tensor_copy(
+                out=x_grouped[slab][:, cols, :].rearrange("p (c i) j -> p c j i", i=4),
+                in_=x_rows[slab][:, :, cols].rearrange("p j (c i) -> p c j i", i=4),
+            )
+
+        def quantise_x(chunk):
+            if not 0 <= chunk < CHUNKS:
+                return
+            slab, c = divmod(chunk, CHUNKS_PER_SLAB)
+            if c == 0:
+                x_codes[slab] = x_pool.tile([P, PIXELS], U32, tag="x_codes", name="x_codes", align_bytes=64)
+                x_scales[slab] = x_pool.tile([P, PIXELS], U8, tag="x_scales", name="x_scales", align_bytes=64)
+            cols = slice(c * CHUNK, (c + 1) * CHUNK)
+            nc.vector.quantize_mx(
+                out=x_codes[slab][:, cols].bitcast(FP8X4),
+                scales=x_scales[slab][:, cols],
+                in_=x_grouped[slab][:, cols, :].rearrange("p n j -> p (n j)"),
+            )
+
+        y = {}
+        sumsq = {}
+        inv_norm = {}
+        factors = {}
+        normed = {}
+        turned_z = {}
+        z_grouped = {}
+        z_codes = {}
+        z_scales = {}
+        scores_acc = {}
+
+        def parts(unit):
+            slab, head = divmod(unit, HEADS)
+            return slab, slab % SIDES, head
+
+        def project(unit):
+            if not 0 <= unit < UNITS:
+                return
+            slab, side, head = parts(unit)
+            rows = slice(head * P, (head + 1) * P)
+            for half in range(HALVES):
+                cols = slice(half * BANK, (half + 1) * BANK)
+                y[unit, half] = psum_y.tile([P, BANK], F32, tag="y", name="y")
+                nc.tensor.matmul_mx(
+                    out=y[unit, half][:],
+                    lhsT=w_codes[side][:, rows].bitcast(FP8X4),
+                    lhsT_scale=w_scales[side][:, rows],
+                    rhs=x_codes[slab][:, cols].bitcast(FP8X4),
+                    rhs_scale=x_scales[slab][:, cols],
+                    start=True,
+                    stop=True,
+                )
+
+        def sum_squares(unit):
+            if not 0 <= unit < UNITS:
+                return
+            slab, side, head = parts(unit)
+            sumsq[unit] = small.tile([P, HALVES], F32, tag="sumsq", name="sumsq")
+            for half in range(HALVES):
+                squares = small.tile([P, BANK], BF16, tag="squares", name="squares")
+                nc.scalar.activation(
+                    out=squares[:],
+                    in_=y[unit, half][:],
+                    func=ACT.Square,
+                    scale=affine[:, side, head, 0:1],
+                    bias=affine[:, side, head, 1:2],
+                    accum_out=sumsq[unit][:, half : half + 1],
+                )
+            inv_norm[unit] = small.tile([P, 1], F32, tag="inv_norm", name="inv_norm")
+            nc.scalar.activation(
+                out=inv_norm[unit][:],
+                in_=sumsq[unit][:, 0:1],
+                func=ACT.Abs_reciprocal_sqrt,
+                bias=sumsq[unit][:, 1:2],
+                scale=1.0,
+            )
+
+        def norm_factors(unit):
+            if not 0 <= unit < UNITS:
+                return
+            slab, side, head = parts(unit)
+            factors[unit] = small.tile([P, 2], F32, tag="factors", name="factors")
+            nc.vector.scalar_tensor_tensor(
+                out=factors[unit][:],
+                in0=inv_norm[unit][:].to_broadcast([P, 2]),
+                scalar=MAX_INV_NORM,
+                in1=affine[:, side, head, :],
+                op0=ALU.min,
+                op1=ALU.mult,
+            )
+
+        def normalise_first_half(unit):
+            if not 0 <= unit < UNITS:
+                return
+            normed[unit] = unit_pool.tile([P, PIXELS], BF16, tag="normed", name="normed")
+            nc.vector.tensor_scalar(
+                out=normed[unit][:, 0:BANK],
+                in0=y[unit, 0][:],
+                scalar1=factors[unit][:, 0:1],
+                scalar2=factors[unit][:, 1:2],
+                op0=ALU.mult,
+                op1=ALU.add,
+            )
+
+        def normalise_second_half(unit):
+            if not 0 <= unit < UNITS:
+                return
+            nc.scalar.activation(
+                out=normed[unit][:, BANK:PIXELS],
+                in_=y[unit, 1][:],
+                func=ACT.Identity,
+                scale=factors[unit][:, 0:1],
+                bias=factors[unit][:, 1:2],
+            )
+
+        def turn(unit):
+            if not 0 <= unit < UNITS:
+                return
+            words = normed[unit][:].bitcast(F32)
+            turned_z[unit] = psum_turned.tile([P, PASSES, 2, P], F32, tag="turned", name="turned_z")
+            for g in range(PASSES):
+                for u in range(2):
+                    first = (2 * g + u) * P
+                    nc.tensor.transpose(turned_z[unit][:, g, u, :], words[:, first : first + P], ident[:])
+
+        def regroup(unit):
+            if not 0 <= unit < UNITS:
+                return
+            z_grouped[unit] = unit_pool.tile(
+                [P, PASSES * P * PACK], BF16, tag="z_grouped", name="z_grouped", align_bytes=64
+            )
+            nc.vector.tensor_copy(
+                out=z_grouped[unit][:].bitcast(F32).rearrange("p (g o u) -> p g o u", g=PASSES, u=2),
+                in_=turned_z[unit][:].rearrange("p g u o -> p g o u"),
+            )
+
+        def quantise(unit):
+            if not 0 <= unit < UNITS:
+                return
+            z_codes[unit] = code_pool.tile([P, PASSES * P], U32, tag="z_codes", name="z_codes", align_bytes=64)
+            z_scales[unit] = code_pool.tile([P, PASSES * P], U8, tag="z_scales", name="z_scales", align_bytes=64)
+            nc.vector.quantize_mx(
+                out=z_codes[unit][:].bitcast(FP8X4), scales=z_scales[unit][:], in_=z_grouped[unit][:]
+            )
+
+        def is_q_unit(unit):
+            return 0 <= unit < UNITS and parts(unit)[1] == 1
+
+        def scores(unit):
+            if not is_q_unit(unit):
+                return
+            k_unit = unit - HEADS
+            scores_acc[unit] = psum_scores.tile([P, P], F32, tag="scores", name="scores_acc")
+            for g in range(PASSES):
+                cols = slice(g * P, (g + 1) * P)
+                nc.tensor.matmul_mx(
+                    out=scores_acc[unit][:],
+                    lhsT=z_codes[unit][:, cols].bitcast(FP8X4),
+                    lhsT_scale=z_scales[unit][:, cols],
+                    rhs=z_codes[k_unit][:, cols].bitcast(FP8X4),
+                    rhs_scale=z_scales[k_unit][:, cols],
+                    start=(g == 0),
+                    stop=(g == PASSES - 1),
+                )
+
+        def store(unit):
+            if not is_q_unit(unit):
+                return
+            slab, side, head = parts(unit)
+            result = small.tile([P, P], F32, tag="result", name="result")
+            nc.vector.tensor_scalar(
+                out=result[:], in0=scores_acc[unit][:], scalar1=temp[:, head : head + 1], scalar2=None, op0=ALU.mult
+            )
+            nc.sync.dma_start(out=out[slab // SIDES, head], in_=result[:])
+
+        turn_weight(0)
+        turn_weight(1)
+        regroup_x(0)
+        quantise_weight(0)
+        regroup_x(1)
+        quantise_x(0)
+        regroup_x(2)
+        quantise_x(1)
+        regroup_x(3)
+        quantise_x(2)
+        quantise_weight(1)
+        quantise_x(3)
+        regroup_x(4)
+
+        for s in range(-1, UNITS + 3):
+            normalise_first_half(s - 1)
+            turn(s - 2)
+            scores(s - 3)
+            project(s + 1)
+            sum_squares(s)
+            normalise_second_half(s - 1)
+            store(s - 3)
+            regroup(s - 2)
+            regroup_x(s + 6)
+            quantise(s - 2)
+            quantise_x(s + 5)
+            norm_factors(s)

@@ -42,12 +42,37 @@ def tile_transposedattention_fusion_pa_t_kernel(
         ctx.enter_context(tc.manual_schedule())
         const = ctx.enter_context(tc.tile_pool(name="const", bufs=1))
         x_pool = ctx.enter_context(tc.tile_pool(name="x_pool", bufs=3))
-        unit_pool = ctx.enter_context(tc.tile_pool(name="unit_pool", bufs=3))
+        unit_pool = ctx.enter_context(tc.tile_pool(name="unit_pool", bufs=4))
         code_pool = ctx.enter_context(tc.tile_pool(name="code_pool", bufs=8))
         small = ctx.enter_context(tc.tile_pool(name="small", bufs=4))
         psum_y = ctx.enter_context(tc.psum_pool(name="psum_y", bufs=5))
-        psum_turned = ctx.enter_context(tc.psum_pool(name="psum_turned", bufs=2))
+        psum_turned = ctx.enter_context(tc.psum_pool(name="psum_turned", bufs=1))
         psum_scores = ctx.enter_context(tc.psum_pool(name="psum_scores", bufs=1))
+
+        w_rows = {}
+        x_rows = {}
+
+        def load_weight(side, w):
+            w_rows[side] = const.tile([P, HEADS * CHANNELS], BF16, name="w_rows%d" % side)
+            nc.sync.dma_start(
+                out=w_rows[side][:].rearrange("o (h c) -> o h c", h=HEADS),
+                in_=w.rearrange("(h o) c -> o h c", o=P),
+            )
+
+        def load_slab(slab, x, pieces):
+            x_rows[slab] = const.tile([P, PACK, PIXELS], BF16, name="x_rows%d" % slab)
+            source = x[slab // SIDES].rearrange("(p j) h w -> p j (h w)", j=PACK)
+            for piece in range(pieces):
+                cols = slice(piece * PIXELS // pieces, (piece + 1) * PIXELS // pieces)
+                nc.sync.dma_start(out=x_rows[slab][:, :, cols], in_=source[:, :, cols])
+
+        load_weight(0, k_w)
+        load_weight(1, q_w)
+        load_slab(0, x1, 2)
+        load_slab(1, x2, 1)
+        for b in range(1, BATCH):
+            load_slab(SIDES * b, x1, 1)
+            load_slab(SIDES * b + 1, x2, 1)
 
         vec_rows = const.tile([P, P], BF16, name="vec_rows")
         nc.vector.memset(vec_rows[:], 0.0)
@@ -62,57 +87,11 @@ def tile_transposedattention_fusion_pa_t_kernel(
             out=temp_bf16[:], in_=temperature.rearrange("h a b -> (h a b)").partition_broadcast(P)
         )
 
-        w_rows = {}
-        x_rows = {}
-
-        def load_weight(side, w):
-            w_rows[side] = const.tile([P, HEADS * CHANNELS], BF16, name="w_rows%d" % side)
-            nc.sync.dma_start(
-                out=w_rows[side][:].rearrange("o (h c) -> o h c", h=HEADS),
-                in_=w.rearrange("(h o) c -> o h c", o=P),
-            )
-
-        def load_slab(slab, x):
-            x_rows[slab] = const.tile([P, PACK, PIXELS], BF16, name="x_rows%d" % slab)
-            nc.sync.dma_start(
-                out=x_rows[slab][:],
-                in_=x[slab // SIDES].rearrange("(p j) h w -> p j (h w)", j=PACK),
-            )
-
-        load_weight(0, k_w)
-        load_slab(0, x1)
-        load_weight(1, q_w)
-        load_slab(1, x2)
-        for b in range(1, BATCH):
-            load_slab(SIDES * b, x1)
-            load_slab(SIDES * b + 1, x2)
-
         warm = const.tile([P, 1], F32, name="warm")
         nc.scalar.activation(out=warm[:], in_=one[:], func=ACT.Abs_reciprocal_sqrt)
 
         ident = const.tile([P, P], F32, name="ident")
         make_identity(nc, ident[:])
-
-        vec_rows_f32 = const.tile([P, P], F32, name="vec_rows_f32")
-        nc.vector.tensor_copy(out=vec_rows_f32[:], in_=vec_rows[:])
-        vec_turned = psum_scores.tile([P, P], F32, tag="scores", name="vec_turned")
-        nc.tensor.transpose(vec_turned[:], vec_rows_f32[:], ident[:])
-        vec_cols = const.tile([P, SIDES, 3, HEADS], F32, name="vec_cols")
-        nc.vector.tensor_copy(
-            out=vec_cols[:].rearrange("o s v h -> o (s v h)"), in_=vec_turned[:, 0 : SIDES * 3 * HEADS]
-        )
-        affine = const.tile([P, SIDES, HEADS, 2], F32, name="affine")
-        nc.vector.tensor_scalar(
-            out=affine[:, :, :, 0], in0=vec_cols[:, :, 1, :], scalar1=INV_STD, scalar2=None, op0=ALU.mult
-        )
-        nc.vector.tensor_tensor(
-            out=affine[:, :, :, 1], in0=vec_cols[:, :, 0, :], in1=affine[:, :, :, 0], op=ALU.mult
-        )
-        nc.vector.tensor_tensor(
-            out=affine[:, :, :, 1], in0=affine[:, :, :, 1], in1=vec_cols[:, :, 2, :], op=ALU.add
-        )
-        temp = const.tile([P, HEADS], F32, name="temp")
-        nc.vector.tensor_copy(out=temp[:], in_=temp_bf16[:])
 
         w_grouped = {}
         w_codes = {}
@@ -125,7 +104,7 @@ def tile_transposedattention_fusion_pa_t_kernel(
             )
             grouped_words = w_grouped[side][:].bitcast(F32).rearrange("p (h o u) -> p h o u", h=HEADS, u=2)
             for pair in range(HEADS // 2):
-                turned = psum_turned.tile([P, 2, 2, P], F32, tag="turned", name="w_turned")
+                turned = psum_turned.tile([P, 2, 2, P], F32, tag="turned%d" % pair, name="w_turned")
                 for i in range(2):
                     for u in range(2):
                         nc.tensor.transpose(turned[:, i, u, :], words[:, 2 * pair + i, u, :], ident[:])
@@ -140,6 +119,29 @@ def tile_transposedattention_fusion_pa_t_kernel(
             nc.vector.quantize_mx(
                 out=w_codes[side][:].bitcast(FP8X4), scales=w_scales[side][:], in_=w_grouped[side][:]
             )
+
+        affine = const.tile([P, SIDES, HEADS, 2], F32, name="affine")
+        temp = const.tile([P, HEADS], F32, name="temp")
+
+        def channel_numbers():
+            vec_rows_f32 = const.tile([P, P], F32, name="vec_rows_f32")
+            nc.vector.tensor_copy(out=vec_rows_f32[:], in_=vec_rows[:])
+            vec_turned = psum_scores.tile([P, P], F32, tag="scores", name="vec_turned")
+            nc.tensor.transpose(vec_turned[:], vec_rows_f32[:], ident[:])
+            vec_cols = const.tile([P, SIDES, 3, HEADS], F32, name="vec_cols")
+            nc.vector.tensor_copy(
+                out=vec_cols[:].rearrange("o s v h -> o (s v h)"), in_=vec_turned[:, 0 : SIDES * 3 * HEADS]
+            )
+            nc.vector.tensor_scalar(
+                out=affine[:, :, :, 0], in0=vec_cols[:, :, 1, :], scalar1=INV_STD, scalar2=None, op0=ALU.mult
+            )
+            nc.vector.tensor_tensor(
+                out=affine[:, :, :, 1], in0=vec_cols[:, :, 0, :], in1=affine[:, :, :, 0], op=ALU.mult
+            )
+            nc.vector.tensor_tensor(
+                out=affine[:, :, :, 1], in0=affine[:, :, :, 1], in1=vec_cols[:, :, 2, :], op=ALU.add
+            )
+            nc.vector.tensor_copy(out=temp[:], in_=temp_bf16[:])
 
         x_grouped = {}
         x_codes = {}
@@ -272,22 +274,25 @@ def tile_transposedattention_fusion_pa_t_kernel(
             if not 0 <= unit < UNITS:
                 return
             words = normed[unit][:].bitcast(F32)
-            turned_z[unit] = psum_turned.tile([P, PASSES, 2, P], F32, tag="turned", name="turned_z")
             for g in range(PASSES):
+                turned_z[unit, g] = psum_turned.tile([P, 2, P], F32, tag="turned%d" % g, name="turned_z")
                 for u in range(2):
                     first = (2 * g + u) * P
-                    nc.tensor.transpose(turned_z[unit][:, g, u, :], words[:, first : first + P], ident[:])
+                    nc.tensor.transpose(turned_z[unit, g][:, u, :], words[:, first : first + P], ident[:])
 
-        def regroup(unit):
+        def regroup(unit, g):
             if not 0 <= unit < UNITS:
                 return
-            z_grouped[unit] = unit_pool.tile(
-                [P, PASSES * P * PACK], BF16, tag="z_grouped", name="z_grouped", align_bytes=64
-            )
-            nc.vector.tensor_copy(
-                out=z_grouped[unit][:].bitcast(F32).rearrange("p (g o u) -> p g o u", g=PASSES, u=2),
-                in_=turned_z[unit][:].rearrange("p g u o -> p g o u"),
-            )
+            if g == 0:
+                z_grouped[unit] = unit_pool.tile(
+                    [P, PASSES * P * PACK], BF16, tag="z_grouped", name="z_grouped", align_bytes=64
+                )
+            grouped_words = z_grouped[unit][:].bitcast(F32).rearrange("p (g o u) -> p g o u", g=PASSES, u=2)
+            turned_words = turned_z[unit, g][:].rearrange("p u o -> p o u")
+            if g == 0:
+                nc.scalar.copy(out=grouped_words[:, g, :, :], in_=turned_words)
+            else:
+                nc.vector.tensor_copy(out=grouped_words[:, g, :, :], in_=turned_words)
 
         def quantise(unit):
             if not 0 <= unit < UNITS:
@@ -330,28 +335,30 @@ def tile_transposedattention_fusion_pa_t_kernel(
 
         turn_weight(0)
         turn_weight(1)
+        channel_numbers()
         regroup_x(0)
-        quantise_weight(0)
         regroup_x(1)
+        quantise_weight(0)
         quantise_x(0)
-        regroup_x(2)
         quantise_x(1)
+        regroup_x(2)
         regroup_x(3)
         quantise_x(2)
-        quantise_weight(1)
         quantise_x(3)
+        quantise_weight(1)
         regroup_x(4)
 
-        for s in range(-1, UNITS + 3):
+        for s in range(-1, UNITS + 4):
             normalise_first_half(s - 1)
             turn(s - 2)
-            scores(s - 3)
+            scores(s - 4)
             project(s + 1)
             sum_squares(s)
+            regroup(s - 2, 0)
             normalise_second_half(s - 1)
-            store(s - 3)
-            regroup(s - 2)
-            regroup_x(s + 6)
-            quantise(s - 2)
-            quantise_x(s + 5)
+            quantise(s - 3)
             norm_factors(s)
+            regroup_x(s + 6)
+            regroup(s - 2, 1)
+            quantise_x(s + 5)
+            store(s - 4)

@@ -190,39 +190,42 @@ def tile_transposedattention_fusion_pa_t_kernel(
             slab, head = divmod(unit, HEADS)
             return slab, slab % SIDES, head
 
-        def project(unit):
+        def project(unit, half):
             if not 0 <= unit < UNITS:
                 return
             slab, side, head = parts(unit)
             rows = slice(head * P, (head + 1) * P)
-            for half in range(HALVES):
-                cols = slice(half * BANK, (half + 1) * BANK)
-                y[unit, half] = psum_y.tile([P, BANK], F32, tag="y", name="y")
-                nc.tensor.matmul_mx(
-                    out=y[unit, half][:],
-                    lhsT=w_codes[side][:, rows].bitcast(FP8X4),
-                    lhsT_scale=w_scales[side][:, rows],
-                    rhs=x_codes[slab][:, cols].bitcast(FP8X4),
-                    rhs_scale=x_scales[slab][:, cols],
-                    start=True,
-                    stop=True,
-                )
+            cols = slice(half * BANK, (half + 1) * BANK)
+            y[unit, half] = psum_y.tile([P, BANK], F32, tag="y", name="y")
+            nc.tensor.matmul_mx(
+                out=y[unit, half][:],
+                lhsT=w_codes[side][:, rows].bitcast(FP8X4),
+                lhsT_scale=w_scales[side][:, rows],
+                rhs=x_codes[slab][:, cols].bitcast(FP8X4),
+                rhs_scale=x_scales[slab][:, cols],
+                start=True,
+                stop=True,
+            )
 
-        def sum_squares(unit):
+        def sum_squares(unit, half):
             if not 0 <= unit < UNITS:
                 return
             slab, side, head = parts(unit)
-            sumsq[unit] = small.tile([P, HALVES], F32, tag="sumsq", name="sumsq")
-            for half in range(HALVES):
-                squares = small.tile([P, BANK], BF16, tag="squares", name="squares")
-                nc.scalar.activation(
-                    out=squares[:],
-                    in_=y[unit, half][:],
-                    func=ACT.Square,
-                    scale=affine[:, side, head, 0:1],
-                    bias=affine[:, side, head, 1:2],
-                    accum_out=sumsq[unit][:, half : half + 1],
-                )
+            if half == 0:
+                sumsq[unit] = small.tile([P, HALVES], F32, tag="sumsq", name="sumsq")
+            squares = small.tile([P, BANK], BF16, tag="squares", name="squares")
+            nc.scalar.activation(
+                out=squares[:],
+                in_=y[unit, half][:],
+                func=ACT.Square,
+                scale=affine[:, side, head, 0:1],
+                bias=affine[:, side, head, 1:2],
+                accum_out=sumsq[unit][:, half : half + 1],
+            )
+
+        def inverse_norm(unit):
+            if not 0 <= unit < UNITS:
+                return
             inv_norm[unit] = small.tile([P, 1], F32, tag="inv_norm", name="inv_norm")
             nc.scalar.activation(
                 out=inv_norm[unit][:],
@@ -350,12 +353,15 @@ def tile_transposedattention_fusion_pa_t_kernel(
 
         for s in range(-1, UNITS + 4):
             normalise_first_half(s - 1)
+            project(s + 1, 0)
             turn(s - 2)
             scores(s - 4)
-            project(s + 1)
-            sum_squares(s)
-            regroup(s - 2, 0)
+            project(s + 1, 1)
+            sum_squares(s, 0)
             normalise_second_half(s - 1)
+            sum_squares(s, 1)
+            inverse_norm(s)
+            regroup(s - 2, 0)
             quantise(s - 3)
             norm_factors(s)
             regroup_x(s + 6)

@@ -24,9 +24,12 @@ HALVES = PIXELS // BANK
 PASSES = PIXELS // (P * PACK)
 SLABS = BATCH * SIDES
 UNITS = SLABS * HEADS
-CHUNK = 256
+PAIRS = UNITS // 2
+PAIRS_PER_SLAB = HEADS // 2
+CHUNK = BANK
 CHUNKS_PER_SLAB = PIXELS // CHUNK
 CHUNKS = SLABS * CHUNKS_PER_SLAB
+UNIT_WORDS = PASSES * P
 BN_EPS = 1e-5
 INV_STD = 1.0 / math.sqrt(1.0 + BN_EPS)
 MAX_INV_NORM = 1e12
@@ -41,9 +44,10 @@ def tile_transposedattention_fusion_pa_t_kernel(
     with ExitStack() as ctx:
         ctx.enter_context(tc.manual_schedule())
         const = ctx.enter_context(tc.tile_pool(name="const", bufs=1))
-        x_pool = ctx.enter_context(tc.tile_pool(name="x_pool", bufs=3))
-        unit_pool = ctx.enter_context(tc.tile_pool(name="unit_pool", bufs=4))
-        code_pool = ctx.enter_context(tc.tile_pool(name="code_pool", bufs=8))
+        x_stage = ctx.enter_context(tc.tile_pool(name="x_stage", bufs=2))
+        x_code_pool = ctx.enter_context(tc.tile_pool(name="x_code_pool", bufs=3))
+        unit_pool = ctx.enter_context(tc.tile_pool(name="unit_pool", bufs=3))
+        code_pool = ctx.enter_context(tc.tile_pool(name="code_pool", bufs=4))
         small = ctx.enter_context(tc.tile_pool(name="small", bufs=4))
         psum_y = ctx.enter_context(tc.psum_pool(name="psum_y", bufs=5))
         psum_turned = ctx.enter_context(tc.psum_pool(name="psum_turned", bufs=1))
@@ -66,26 +70,26 @@ def tile_transposedattention_fusion_pa_t_kernel(
                 cols = slice(piece * PIXELS // pieces, (piece + 1) * PIXELS // pieces)
                 nc.sync.dma_start(out=x_rows[slab][:, :, cols], in_=source[:, :, cols])
 
-        load_weight(0, k_w)
-        load_weight(1, q_w)
-        load_slab(0, x1, 2)
-        load_slab(1, x2, 1)
-        for b in range(1, BATCH):
-            load_slab(SIDES * b, x1, 1)
-            load_slab(SIDES * b + 1, x2, 1)
-
         vec_rows = const.tile([P, P], BF16, name="vec_rows")
         nc.vector.memset(vec_rows[:], 0.0)
         one = const.tile([P, 1], F32, name="one")
         nc.vector.memset(one[:], 1.0)
+
+        load_weight(0, k_w)
+        load_slab(0, x1, CHUNKS_PER_SLAB)
         for v, vec in enumerate((k_b, bnk_w, bnk_b, q_b, bnq_w, bnq_b)):
-            nc.scalar.dma_start(
+            nc.sync.dma_start(
                 out=vec_rows[HEADS * v : HEADS * (v + 1), :], in_=vec.rearrange("(h o) -> h o", o=P)
             )
         temp_bf16 = const.tile([P, HEADS], BF16, name="temp_bf16")
-        nc.scalar.dma_start(
+        nc.sync.dma_start(
             out=temp_bf16[:], in_=temperature.rearrange("h a b -> (h a b)").partition_broadcast(P)
         )
+        load_slab(1, x2, 1)
+        load_weight(1, q_w)
+        for b in range(1, BATCH):
+            load_slab(SIDES * b, x1, 1)
+            load_slab(SIDES * b + 1, x2, 1)
 
         warm = const.tile([P, 1], F32, name="warm")
         nc.scalar.activation(out=warm[:], in_=one[:], func=ACT.Abs_reciprocal_sqrt)
@@ -93,35 +97,33 @@ def tile_transposedattention_fusion_pa_t_kernel(
         ident = const.tile([P, P], F32, name="ident")
         make_identity(nc, ident[:])
 
-        w_grouped = {}
         w_codes = {}
         w_scales = {}
 
-        def turn_weight(side):
+        def prepare_weight(side, copy_out):
             words = w_rows[side][:].bitcast(F32).rearrange("o (h p u) -> o h u p", h=HEADS, u=2)
-            w_grouped[side] = const.tile(
-                [P, HEADS * P * PACK], BF16, name="w_grouped%d" % side, align_bytes=64
-            )
-            grouped_words = w_grouped[side][:].bitcast(F32).rearrange("p (h o u) -> p h o u", h=HEADS, u=2)
+            w_grouped = const.tile([P, HEADS * P * PACK], BF16, name="w_grouped%d" % side, align_bytes=64)
+            grouped_words = w_grouped[:].bitcast(F32).rearrange("p (h o u) -> p h o u", h=HEADS, u=2)
             for pair in range(HEADS // 2):
                 turned = psum_turned.tile([P, 2, 2, P], F32, tag="turned%d" % pair, name="w_turned")
                 for i in range(2):
                     for u in range(2):
                         nc.tensor.transpose(turned[:, i, u, :], words[:, 2 * pair + i, u, :], ident[:])
-                nc.scalar.copy(
+                copy_out(
                     out=grouped_words[:, 2 * pair : 2 * pair + 2, :, :],
                     in_=turned[:].rearrange("p i u o -> p i o u"),
                 )
-
-        def quantise_weight(side):
             w_codes[side] = const.tile([P, CHANNELS], U32, name="w_codes%d" % side, align_bytes=64)
             w_scales[side] = const.tile([P, CHANNELS], U8, name="w_scales%d" % side, align_bytes=64)
+            return w_grouped
+
+        def quantise_weight(side, w_grouped):
             nc.vector.quantize_mx(
-                out=w_codes[side][:].bitcast(FP8X4), scales=w_scales[side][:], in_=w_grouped[side][:]
+                out=w_codes[side][:].bitcast(FP8X4), scales=w_scales[side][:], in_=w_grouped[:]
             )
 
         affine = const.tile([P, SIDES, HEADS, 2], F32, name="affine")
-        temp = const.tile([P, HEADS], F32, name="temp")
+        temp_full = const.tile([P, HEADS, P], F32, name="temp_full")
 
         def channel_numbers():
             vec_rows_f32 = const.tile([P, P], F32, name="vec_rows_f32")
@@ -141,7 +143,9 @@ def tile_transposedattention_fusion_pa_t_kernel(
             nc.vector.tensor_tensor(
                 out=affine[:, :, :, 1], in0=affine[:, :, :, 1], in1=vec_cols[:, :, 2, :], op=ALU.add
             )
-            nc.vector.tensor_copy(out=temp[:], in_=temp_bf16[:])
+
+        def spread_temperature():
+            nc.vector.tensor_copy(out=temp_full[:], in_=temp_bf16[:].unsqueeze(2).to_broadcast([P, HEADS, P]))
 
         x_grouped = {}
         x_codes = {}
@@ -151,14 +155,10 @@ def tile_transposedattention_fusion_pa_t_kernel(
             if not 0 <= chunk < CHUNKS:
                 return
             slab, c = divmod(chunk, CHUNKS_PER_SLAB)
-            if c == 0:
-                x_grouped[slab] = x_pool.tile(
-                    [P, PIXELS, PACK], BF16, tag="x_grouped", name="x_grouped", align_bytes=64
-                )
-            cols = slice(c * CHUNK, (c + 1) * CHUNK)
+            x_grouped[chunk] = x_stage.tile([P, CHUNK, PACK], BF16, tag="x_grouped", name="x_grouped", align_bytes=64)
             nc.vector.tensor_copy(
-                out=x_grouped[slab][:, cols, :].rearrange("p (c i) j -> p c j i", i=4),
-                in_=x_rows[slab][:, :, cols].rearrange("p j (c i) -> p c j i", i=4),
+                out=x_grouped[chunk][:].rearrange("p (c i) j -> p c j i", i=4),
+                in_=x_rows[slab][:, :, c * CHUNK : (c + 1) * CHUNK].rearrange("p j (c i) -> p c j i", i=4),
             )
 
         def quantise_x(chunk):
@@ -166,13 +166,13 @@ def tile_transposedattention_fusion_pa_t_kernel(
                 return
             slab, c = divmod(chunk, CHUNKS_PER_SLAB)
             if c == 0:
-                x_codes[slab] = x_pool.tile([P, PIXELS], U32, tag="x_codes", name="x_codes", align_bytes=64)
-                x_scales[slab] = x_pool.tile([P, PIXELS], U8, tag="x_scales", name="x_scales", align_bytes=64)
+                x_codes[slab] = x_code_pool.tile([P, PIXELS], U32, tag="x_codes", name="x_codes", align_bytes=64)
+                x_scales[slab] = x_code_pool.tile([P, PIXELS], U8, tag="x_scales", name="x_scales", align_bytes=64)
             cols = slice(c * CHUNK, (c + 1) * CHUNK)
             nc.vector.quantize_mx(
                 out=x_codes[slab][:, cols].bitcast(FP8X4),
                 scales=x_scales[slab][:, cols],
-                in_=x_grouped[slab][:, cols, :].rearrange("p n j -> p (n j)"),
+                in_=x_grouped[chunk][:].rearrange("p n j -> p (n j)"),
             )
 
         y = {}
@@ -249,29 +249,20 @@ def tile_transposedattention_fusion_pa_t_kernel(
                 op1=ALU.mult,
             )
 
-        def normalise_first_half(unit):
+        def normalise(unit, half):
             if not 0 <= unit < UNITS:
                 return
-            normed[unit] = unit_pool.tile([P, PIXELS], BF16, tag="normed", name="normed")
-            nc.vector.tensor_scalar(
-                out=normed[unit][:, 0:BANK],
-                in0=y[unit, 0][:],
-                scalar1=factors[unit][:, 0:1],
-                scalar2=factors[unit][:, 1:2],
-                op0=ALU.mult,
-                op1=ALU.add,
-            )
-
-        def normalise_second_half(unit):
-            if not 0 <= unit < UNITS:
-                return
-            nc.scalar.activation(
-                out=normed[unit][:, BANK:PIXELS],
-                in_=y[unit, 1][:],
-                func=ACT.Identity,
-                scale=factors[unit][:, 0:1],
-                bias=factors[unit][:, 1:2],
-            )
+            scale = factors[unit][:, 0:1]
+            shift = factors[unit][:, 1:2]
+            if half == 0:
+                normed[unit] = unit_pool.tile([P, PIXELS], BF16, tag="normed", name="normed")
+                nc.vector.tensor_scalar(
+                    out=normed[unit][:, 0:BANK], in0=y[unit, 0][:], scalar1=scale, scalar2=shift, op0=ALU.mult, op1=ALU.add
+                )
+            else:
+                nc.scalar.activation(
+                    out=normed[unit][:, BANK:PIXELS], in_=y[unit, 1][:], func=ACT.Identity, scale=scale, bias=shift
+                )
 
         def turn(unit):
             if not 0 <= unit < UNITS:
@@ -286,85 +277,99 @@ def tile_transposedattention_fusion_pa_t_kernel(
         def regroup(unit, g):
             if not 0 <= unit < UNITS:
                 return
-            if g == 0:
-                z_grouped[unit] = unit_pool.tile(
-                    [P, PASSES * P * PACK], BF16, tag="z_grouped", name="z_grouped", align_bytes=64
+            pair, i = divmod(unit, 2)
+            if i == 0 and g == 0:
+                z_grouped[pair] = unit_pool.tile(
+                    [P, 2 * UNIT_WORDS * PACK], BF16, tag="z_grouped", name="z_grouped", align_bytes=64
                 )
-            grouped_words = z_grouped[unit][:].bitcast(F32).rearrange("p (g o u) -> p g o u", g=PASSES, u=2)
+            grouped_words = z_grouped[pair][:].bitcast(F32).rearrange("p (i g o u) -> p i g o u", i=2, g=PASSES, u=2)
             turned_words = turned_z[unit, g][:].rearrange("p u o -> p o u")
             if g == 0:
-                nc.scalar.copy(out=grouped_words[:, g, :, :], in_=turned_words)
+                nc.scalar.copy(out=grouped_words[:, i, g, :, :], in_=turned_words)
             else:
-                nc.vector.tensor_copy(out=grouped_words[:, g, :, :], in_=turned_words)
+                nc.vector.tensor_copy(out=grouped_words[:, i, g, :, :], in_=turned_words)
 
-        def quantise(unit):
-            if not 0 <= unit < UNITS:
+        def quantise_pair(pair):
+            if not 0 <= pair < PAIRS:
                 return
-            z_codes[unit] = code_pool.tile([P, PASSES * P], U32, tag="z_codes", name="z_codes", align_bytes=64)
-            z_scales[unit] = code_pool.tile([P, PASSES * P], U8, tag="z_scales", name="z_scales", align_bytes=64)
+            z_codes[pair] = code_pool.tile([P, 2 * UNIT_WORDS], U32, tag="z_codes", name="z_codes", align_bytes=64)
+            z_scales[pair] = code_pool.tile([P, 2 * UNIT_WORDS], U8, tag="z_scales", name="z_scales", align_bytes=64)
             nc.vector.quantize_mx(
-                out=z_codes[unit][:].bitcast(FP8X4), scales=z_scales[unit][:], in_=z_grouped[unit][:]
+                out=z_codes[pair][:].bitcast(FP8X4), scales=z_scales[pair][:], in_=z_grouped[pair][:]
             )
 
-        def is_q_unit(unit):
-            return 0 <= unit < UNITS and parts(unit)[1] == 1
+        def is_q_pair(pair):
+            return 0 <= pair < PAIRS and (pair // PAIRS_PER_SLAB) % SIDES == 1
 
-        def scores(unit):
-            if not is_q_unit(unit):
+        def scores(pair):
+            if not is_q_pair(pair):
                 return
-            k_unit = unit - HEADS
-            scores_acc[unit] = psum_scores.tile([P, P], F32, tag="scores", name="scores_acc")
-            for g in range(PASSES):
-                cols = slice(g * P, (g + 1) * P)
-                nc.tensor.matmul_mx(
-                    out=scores_acc[unit][:],
-                    lhsT=z_codes[unit][:, cols].bitcast(FP8X4),
-                    lhsT_scale=z_scales[unit][:, cols],
-                    rhs=z_codes[k_unit][:, cols].bitcast(FP8X4),
-                    rhs_scale=z_scales[k_unit][:, cols],
-                    start=(g == 0),
-                    stop=(g == PASSES - 1),
-                )
+            k_pair = pair - PAIRS_PER_SLAB
+            scores_acc[pair] = psum_scores.tile([P, 2, P], F32, tag="scores", name="scores_acc")
+            for i in range(2):
+                for g in range(PASSES):
+                    cols = slice(i * UNIT_WORDS + g * P, i * UNIT_WORDS + (g + 1) * P)
+                    nc.tensor.matmul_mx(
+                        out=scores_acc[pair][:, i, :],
+                        lhsT=z_codes[pair][:, cols].bitcast(FP8X4),
+                        lhsT_scale=z_scales[pair][:, cols],
+                        rhs=z_codes[k_pair][:, cols].bitcast(FP8X4),
+                        rhs_scale=z_scales[k_pair][:, cols],
+                        start=(g == 0),
+                        stop=(g == PASSES - 1),
+                    )
 
-        def store(unit):
-            if not is_q_unit(unit):
+        def store(pair):
+            if not is_q_pair(pair):
                 return
-            slab, side, head = parts(unit)
-            result = small.tile([P, P], F32, tag="result", name="result")
-            nc.vector.tensor_scalar(
-                out=result[:], in0=scores_acc[unit][:], scalar1=temp[:, head : head + 1], scalar2=None, op0=ALU.mult
+            batch = pair // (SIDES * PAIRS_PER_SLAB)
+            heads = slice(2 * (pair % PAIRS_PER_SLAB), 2 * (pair % PAIRS_PER_SLAB) + 2)
+            result = small.tile([P, 2, P], F32, tag="result", name="result")
+            nc.vector.tensor_tensor(
+                out=result[:], in0=scores_acc[pair][:], in1=temp_full[:, heads, :], op=ALU.mult
             )
-            nc.sync.dma_start(out=out[slab // SIDES, head], in_=result[:])
+            nc.sync.dma_start(out=out[batch, heads].rearrange("h c d -> c h d"), in_=result[:])
 
-        turn_weight(0)
-        turn_weight(1)
-        channel_numbers()
-        regroup_x(0)
-        regroup_x(1)
-        quantise_weight(0)
-        quantise_x(0)
-        quantise_x(1)
-        regroup_x(2)
-        regroup_x(3)
-        quantise_x(2)
-        quantise_x(3)
-        quantise_weight(1)
-        regroup_x(4)
-
-        for s in range(-1, UNITS + 4):
-            normalise_first_half(s - 1)
+        def step(s):
+            even = s % 2 == 0
+            normalise(s - 1, 0)
             project(s + 1, 0)
             turn(s - 2)
-            scores(s - 4)
+            if not even:
+                scores((s - 5) // 2)
             project(s + 1, 1)
             sum_squares(s, 0)
-            normalise_second_half(s - 1)
             sum_squares(s, 1)
+            normalise(s - 1, 1)
             inverse_norm(s)
             regroup(s - 2, 0)
-            quantise(s - 3)
+            if even:
+                quantise_pair((s - 4) // 2)
+            else:
+                regroup_x((s + 5) // 2)
             norm_factors(s)
-            regroup_x(s + 6)
             regroup(s - 2, 1)
-            quantise_x(s + 5)
-            store(s - 4)
+            if even:
+                quantise_x((s + 4) // 2)
+            else:
+                store((s - 5) // 2)
+
+        FIRST_STEP = -1
+        FIRST_Q_STEP = HEADS - 1
+        LAST_STEP = UNITS + 3
+
+        k_grouped = prepare_weight(0, nc.scalar.copy)
+        regroup_x(0)
+        quantise_weight(0, k_grouped)
+        quantise_x(0)
+        regroup_x(1)
+        channel_numbers()
+        quantise_x(1)
+        for s in range(FIRST_STEP, FIRST_Q_STEP - 2):
+            step(s)
+        q_grouped = prepare_weight(1, nc.vector.tensor_copy)
+        step(FIRST_Q_STEP - 2)
+        quantise_weight(1, q_grouped)
+        spread_temperature()
+        for s in range(FIRST_Q_STEP - 1, LAST_STEP + 1):
+            step(s)

@@ -63,33 +63,34 @@ def tile_transposedattention_fusion_pa_t_kernel(
                 in_=w.rearrange("(h o) c -> o h c", o=P),
             )
 
-        def load_slab(slab, x, pieces):
-            x_rows[slab] = const.tile([P, PACK, PIXELS], BF16, name="x_rows%d" % slab)
+        def load_pixels(slab, x, first, count):
+            if first == 0:
+                x_rows[slab] = const.tile([P, PACK, PIXELS], BF16, name="x_rows%d" % slab)
             source = x[slab // SIDES].rearrange("(p j) h w -> p j (h w)", j=PACK)
-            for piece in range(pieces):
-                cols = slice(piece * PIXELS // pieces, (piece + 1) * PIXELS // pieces)
-                nc.sync.dma_start(out=x_rows[slab][:, :, cols], in_=source[:, :, cols])
+            cols = slice(first, first + count)
+            nc.sync.dma_start(out=x_rows[slab][:, :, cols], in_=source[:, :, cols])
 
         vec_rows = const.tile([P, P], BF16, name="vec_rows")
         nc.vector.memset(vec_rows[:], 0.0)
         one = const.tile([P, 1], F32, name="one")
         nc.vector.memset(one[:], 1.0)
 
-        load_weight(0, k_w)
-        load_slab(0, x1, CHUNKS_PER_SLAB)
+        load_pixels(0, x1, 0, CHUNK)
         for v, vec in enumerate((k_b, bnk_w, bnk_b, q_b, bnq_w, bnq_b)):
             nc.sync.dma_start(
                 out=vec_rows[HEADS * v : HEADS * (v + 1), :], in_=vec.rearrange("(h o) -> h o", o=P)
             )
+        load_weight(0, k_w)
+        load_pixels(0, x1, CHUNK, PIXELS - CHUNK)
         temp_bf16 = const.tile([P, HEADS], BF16, name="temp_bf16")
         nc.sync.dma_start(
             out=temp_bf16[:], in_=temperature.rearrange("h a b -> (h a b)").partition_broadcast(P)
         )
-        load_slab(1, x2, 1)
+        load_pixels(1, x2, 0, PIXELS)
         load_weight(1, q_w)
         for b in range(1, BATCH):
-            load_slab(SIDES * b, x1, 1)
-            load_slab(SIDES * b + 1, x2, 1)
+            load_pixels(SIDES * b, x1, 0, PIXELS)
+            load_pixels(SIDES * b + 1, x2, 0, PIXELS)
 
         warm = const.tile([P, 1], F32, name="warm")
         nc.scalar.activation(out=warm[:], in_=one[:], func=ACT.Abs_reciprocal_sqrt)
@@ -358,12 +359,12 @@ def tile_transposedattention_fusion_pa_t_kernel(
         FIRST_Q_STEP = HEADS - 1
         LAST_STEP = UNITS + 3
 
-        k_grouped = prepare_weight(0, nc.scalar.copy)
         regroup_x(0)
-        quantise_weight(0, k_grouped)
-        quantise_x(0)
-        regroup_x(1)
         channel_numbers()
+        quantise_x(0)
+        k_grouped = prepare_weight(0, nc.scalar.copy)
+        regroup_x(1)
+        quantise_weight(0, k_grouped)
         quantise_x(1)
         for s in range(FIRST_STEP, FIRST_Q_STEP - 2):
             step(s)

@@ -30,6 +30,10 @@ CHUNK = BANK
 CHUNKS_PER_SLAB = PIXELS // CHUNK
 CHUNKS = SLABS * CHUNKS_PER_SLAB
 UNIT_WORDS = PASSES * P
+HALF_WORDS = 2
+RUN = 4
+GPSIMD_PIXELS = 192
+VECTOR_PIXELS = CHUNK - GPSIMD_PIXELS
 BN_EPS = 1e-5
 INV_STD = 1.0 / math.sqrt(1.0 + BN_EPS)
 MAX_INV_NORM = 1e12
@@ -44,7 +48,7 @@ def tile_transposedattention_fusion_pa_t_kernel(
     with ExitStack() as ctx:
         ctx.enter_context(tc.manual_schedule())
         const = ctx.enter_context(tc.tile_pool(name="const", bufs=1))
-        x_stage = ctx.enter_context(tc.tile_pool(name="x_stage", bufs=2))
+        x_stage = ctx.enter_context(tc.tile_pool(name="x_stage", bufs=1))
         x_code_pool = ctx.enter_context(tc.tile_pool(name="x_code_pool", bufs=3))
         unit_pool = ctx.enter_context(tc.tile_pool(name="unit_pool", bufs=3))
         code_pool = ctx.enter_context(tc.tile_pool(name="code_pool", bufs=4))
@@ -55,19 +59,21 @@ def tile_transposedattention_fusion_pa_t_kernel(
 
         w_rows = {}
         x_rows = {}
-
-        def load_weight(side, w):
+        for side in range(SIDES):
             w_rows[side] = const.tile([P, HEADS * CHANNELS], BF16, name="w_rows%d" % side)
+        for slab in range(SLABS):
+            x_rows[slab] = const.tile([P, PACK, PIXELS], BF16, name="x_rows%d" % slab)
+
+        def load_weight(side, pair):
+            heads = slice(2 * pair, 2 * pair + 2)
             nc.sync.dma_start(
-                out=w_rows[side][:].rearrange("o (h c) -> o h c", h=HEADS),
-                in_=w.rearrange("(h o) c -> o h c", o=P),
+                out=w_rows[side][:].rearrange("o (h c) -> o h c", h=HEADS)[:, heads, :],
+                in_=(k_w, q_w)[side].rearrange("(h o) c -> o h c", o=P)[:, heads, :],
             )
 
-        def load_pixels(slab, x, first, count):
-            if first == 0:
-                x_rows[slab] = const.tile([P, PACK, PIXELS], BF16, name="x_rows%d" % slab)
-            source = x[slab // SIDES].rearrange("(p j) h w -> p j (h w)", j=PACK)
-            cols = slice(first, first + count)
+        def load_x(slab, first_chunk, chunks):
+            cols = slice(first_chunk * CHUNK, (first_chunk + chunks) * CHUNK)
+            source = (x1, x2)[slab % SIDES][slab // SIDES].rearrange("(p j) h w -> p j (h w)", j=PACK)
             nc.sync.dma_start(out=x_rows[slab][:, :, cols], in_=source[:, :, cols])
 
         vec_rows = const.tile([P, P], BF16, name="vec_rows")
@@ -75,22 +81,23 @@ def tile_transposedattention_fusion_pa_t_kernel(
         one = const.tile([P, 1], F32, name="one")
         nc.vector.memset(one[:], 1.0)
 
-        load_pixels(0, x1, 0, CHUNK)
+        load_weight(0, 0)
+        load_x(0, 0, 1)
         for v, vec in enumerate((k_b, bnk_w, bnk_b, q_b, bnq_w, bnq_b)):
             nc.sync.dma_start(
                 out=vec_rows[HEADS * v : HEADS * (v + 1), :], in_=vec.rearrange("(h o) -> h o", o=P)
             )
-        load_weight(0, k_w)
-        load_pixels(0, x1, CHUNK, PIXELS - CHUNK)
+        load_weight(0, 1)
+        load_x(0, 1, 1)
+        load_x(1, 0, CHUNKS_PER_SLAB)
+        load_weight(1, 0)
+        load_weight(1, 1)
         temp_bf16 = const.tile([P, HEADS], BF16, name="temp_bf16")
         nc.sync.dma_start(
             out=temp_bf16[:], in_=temperature.rearrange("h a b -> (h a b)").partition_broadcast(P)
         )
-        load_pixels(1, x2, 0, PIXELS)
-        load_weight(1, q_w)
-        for b in range(1, BATCH):
-            load_pixels(SIDES * b, x1, 0, PIXELS)
-            load_pixels(SIDES * b + 1, x2, 0, PIXELS)
+        for slab in range(SIDES, SLABS):
+            load_x(slab, 0, CHUNKS_PER_SLAB)
 
         warm = const.tile([P, 1], F32, name="warm")
         nc.scalar.activation(out=warm[:], in_=one[:], func=ACT.Abs_reciprocal_sqrt)
@@ -98,29 +105,33 @@ def tile_transposedattention_fusion_pa_t_kernel(
         ident = const.tile([P, P], F32, name="ident")
         make_identity(nc, ident[:])
 
+        w_grouped = {}
         w_codes = {}
         w_scales = {}
-
-        def prepare_weight(side, copy_out):
-            words = w_rows[side][:].bitcast(F32).rearrange("o (h p u) -> o h u p", h=HEADS, u=2)
-            w_grouped = const.tile([P, HEADS * P * PACK], BF16, name="w_grouped%d" % side, align_bytes=64)
-            grouped_words = w_grouped[:].bitcast(F32).rearrange("p (h o u) -> p h o u", h=HEADS, u=2)
-            for pair in range(HEADS // 2):
-                turned = psum_turned.tile([P, 2, 2, P], F32, tag="turned%d" % pair, name="w_turned")
-                for i in range(2):
-                    for u in range(2):
-                        nc.tensor.transpose(turned[:, i, u, :], words[:, 2 * pair + i, u, :], ident[:])
-                copy_out(
-                    out=grouped_words[:, 2 * pair : 2 * pair + 2, :, :],
-                    in_=turned[:].rearrange("p i u o -> p i o u"),
-                )
+        for side in range(SIDES):
+            w_grouped[side] = const.tile([P, HEADS * P * PACK], BF16, name="w_grouped%d" % side, align_bytes=64)
             w_codes[side] = const.tile([P, CHANNELS], U32, name="w_codes%d" % side, align_bytes=64)
             w_scales[side] = const.tile([P, CHANNELS], U8, name="w_scales%d" % side, align_bytes=64)
-            return w_grouped
 
-        def quantise_weight(side, w_grouped):
+        def turn_weight(side, pair, copy_out):
+            words = w_rows[side][:].bitcast(F32).rearrange("o (h p u) -> o h u p", h=HEADS, u=HALF_WORDS)
+            grouped_words = w_grouped[side][:].bitcast(F32).rearrange("p (h o u) -> p h o u", h=HEADS, u=HALF_WORDS)
+            turned = psum_turned.tile([P, 2, HALF_WORDS, P], F32, tag="turned%d" % pair, name="w_turned")
+            for i in range(2):
+                for u in range(HALF_WORDS):
+                    nc.tensor.transpose(turned[:, i, u, :], words[:, 2 * pair + i, u, :], ident[:])
+            copy_out(
+                out=grouped_words[:, 2 * pair : 2 * pair + 2, :, :],
+                in_=turned[:].rearrange("p i u o -> p i o u"),
+            )
+
+        def quantise_weight(side, pair):
+            rows = slice(2 * pair * P, 2 * (pair + 1) * P)
+            values = slice(2 * pair * P * PACK, 2 * (pair + 1) * P * PACK)
             nc.vector.quantize_mx(
-                out=w_codes[side][:].bitcast(FP8X4), scales=w_scales[side][:], in_=w_grouped[:]
+                out=w_codes[side][:, rows].bitcast(FP8X4),
+                scales=w_scales[side][:, rows],
+                in_=w_grouped[side][:, values],
             )
 
         affine = const.tile([P, SIDES, HEADS, 2], F32, name="affine")
@@ -128,21 +139,29 @@ def tile_transposedattention_fusion_pa_t_kernel(
 
         def channel_numbers():
             vec_rows_f32 = const.tile([P, P], F32, name="vec_rows_f32")
-            nc.vector.tensor_copy(out=vec_rows_f32[:], in_=vec_rows[:])
+            nc.gpsimd.tensor_scalar(
+                out=vec_rows_f32[:], in0=vec_rows[:], scalar1=1.0, scalar2=0.0, op0=ALU.mult, op1=ALU.add
+            )
             vec_turned = psum_scores.tile([P, P], F32, tag="scores", name="vec_turned")
             nc.tensor.transpose(vec_turned[:], vec_rows_f32[:], ident[:])
             vec_cols = const.tile([P, SIDES, 3, HEADS], F32, name="vec_cols")
-            nc.vector.tensor_copy(
+            nc.scalar.copy(
                 out=vec_cols[:].rearrange("o s v h -> o (s v h)"), in_=vec_turned[:, 0 : SIDES * 3 * HEADS]
+            )
+            scaled_bias = const.tile([P, SIDES, HEADS], F32, name="scaled_bias")
+            nc.vector.scalar_tensor_tensor(
+                out=scaled_bias[:],
+                in0=vec_cols[:, :, 0, :],
+                scalar=INV_STD,
+                in1=vec_cols[:, :, 1, :],
+                op0=ALU.mult,
+                op1=ALU.mult,
             )
             nc.vector.tensor_scalar(
                 out=affine[:, :, :, 0], in0=vec_cols[:, :, 1, :], scalar1=INV_STD, scalar2=None, op0=ALU.mult
             )
             nc.vector.tensor_tensor(
-                out=affine[:, :, :, 1], in0=vec_cols[:, :, 0, :], in1=affine[:, :, :, 0], op=ALU.mult
-            )
-            nc.vector.tensor_tensor(
-                out=affine[:, :, :, 1], in0=affine[:, :, :, 1], in1=vec_cols[:, :, 2, :], op=ALU.add
+                out=affine[:, :, :, 1], in0=scaled_bias[:], in1=vec_cols[:, :, 2, :], op=ALU.add
             )
 
         def spread_temperature():
@@ -152,14 +171,33 @@ def tile_transposedattention_fusion_pa_t_kernel(
         x_codes = {}
         x_scales = {}
 
-        def regroup_x(chunk):
+        def x_grouped_tile(chunk):
+            if chunk not in x_grouped:
+                x_grouped[chunk] = x_stage.tile(
+                    [P, CHUNK, PACK], BF16, tag="x_grouped", name="x_grouped", align_bytes=64
+                )
+            return x_grouped[chunk]
+
+        def regroup_x_gpsimd(chunk):
             if not 0 <= chunk < CHUNKS:
                 return
             slab, c = divmod(chunk, CHUNKS_PER_SLAB)
-            x_grouped[chunk] = x_stage.tile([P, CHUNK, PACK], BF16, tag="x_grouped", name="x_grouped", align_bytes=64)
+            nc.gpsimd.tensor_scalar(
+                out=x_grouped_tile(chunk)[:, VECTOR_PIXELS:CHUNK, :],
+                in0=x_rows[slab][:, :, c * CHUNK + VECTOR_PIXELS : (c + 1) * CHUNK].rearrange("p j n -> p n j"),
+                scalar1=1.0,
+                scalar2=0.0,
+                op0=ALU.mult,
+                op1=ALU.add,
+            )
+
+        def regroup_x_vector(chunk, pixels):
+            if not 0 <= chunk < CHUNKS:
+                return
+            slab, c = divmod(chunk, CHUNKS_PER_SLAB)
             nc.vector.tensor_copy(
-                out=x_grouped[chunk][:].rearrange("p (c i) j -> p c j i", i=4),
-                in_=x_rows[slab][:, :, c * CHUNK : (c + 1) * CHUNK].rearrange("p j (c i) -> p c j i", i=4),
+                out=x_grouped_tile(chunk)[:, 0:pixels, :].rearrange("p (c i) j -> p c j i", i=RUN),
+                in_=x_rows[slab][:, :, c * CHUNK : c * CHUNK + pixels].rearrange("p j (c i) -> p c j i", i=RUN),
             )
 
         def quantise_x(chunk):
@@ -270,9 +308,9 @@ def tile_transposedattention_fusion_pa_t_kernel(
                 return
             words = normed[unit][:].bitcast(F32)
             for g in range(PASSES):
-                turned_z[unit, g] = psum_turned.tile([P, 2, P], F32, tag="turned%d" % g, name="turned_z")
-                for u in range(2):
-                    first = (2 * g + u) * P
+                turned_z[unit, g] = psum_turned.tile([P, HALF_WORDS, P], F32, tag="turned%d" % g, name="turned_z")
+                for u in range(HALF_WORDS):
+                    first = (HALF_WORDS * g + u) * P
                     nc.tensor.transpose(turned_z[unit, g][:, u, :], words[:, first : first + P], ident[:])
 
         def regroup(unit, g):
@@ -283,7 +321,9 @@ def tile_transposedattention_fusion_pa_t_kernel(
                 z_grouped[pair] = unit_pool.tile(
                     [P, 2 * UNIT_WORDS * PACK], BF16, tag="z_grouped", name="z_grouped", align_bytes=64
                 )
-            grouped_words = z_grouped[pair][:].bitcast(F32).rearrange("p (i g o u) -> p i g o u", i=2, g=PASSES, u=2)
+            grouped_words = z_grouped[pair][:].bitcast(F32).rearrange(
+                "p (i g o u) -> p i g o u", i=2, g=PASSES, u=HALF_WORDS
+            )
             turned_words = turned_z[unit, g][:].rearrange("p u o -> p o u")
             if g == 0:
                 nc.scalar.copy(out=grouped_words[:, i, g, :, :], in_=turned_words)
@@ -344,33 +384,39 @@ def tile_transposedattention_fusion_pa_t_kernel(
             normalise(s - 1, 1)
             inverse_norm(s)
             regroup(s - 2, 0)
+            regroup(s - 2, 1)
             if even:
                 quantise_pair((s - 4) // 2)
             else:
-                regroup_x((s + 5) // 2)
+                store((s - 5) // 2)
             norm_factors(s)
-            regroup(s - 2, 1)
             if even:
                 quantise_x((s + 4) // 2)
+                regroup_x_gpsimd((s + 6) // 2)
             else:
-                store((s - 5) // 2)
+                regroup_x_vector((s + 5) // 2, VECTOR_PIXELS)
 
         FIRST_STEP = -1
         FIRST_Q_STEP = HEADS - 1
         LAST_STEP = UNITS + 3
 
-        regroup_x(0)
-        channel_numbers()
+        turn_weight(0, 0, nc.scalar.copy)
+        turn_weight(0, 1, nc.scalar.copy)
+        regroup_x_vector(0, CHUNK)
+        quantise_weight(0, 0)
         quantise_x(0)
-        k_grouped = prepare_weight(0, nc.scalar.copy)
-        regroup_x(1)
-        quantise_weight(0, k_grouped)
+        regroup_x_vector(1, CHUNK)
+        channel_numbers()
         quantise_x(1)
+        regroup_x_gpsimd(2)
+        quantise_weight(0, 1)
         for s in range(FIRST_STEP, FIRST_Q_STEP - 2):
             step(s)
-        q_grouped = prepare_weight(1, nc.vector.tensor_copy)
+        turn_weight(1, 0, nc.vector.tensor_copy)
+        turn_weight(1, 1, nc.vector.tensor_copy)
         step(FIRST_Q_STEP - 2)
-        quantise_weight(1, q_grouped)
+        quantise_weight(1, 0)
+        quantise_weight(1, 1)
         spread_temperature()
         for s in range(FIRST_Q_STEP - 1, LAST_STEP + 1):
             step(s)

@@ -24,16 +24,12 @@ HALVES = PIXELS // BANK
 PASSES = PIXELS // (P * PACK)
 SLABS = BATCH * SIDES
 UNITS = SLABS * HEADS
-PAIRS = UNITS // 2
-PAIRS_PER_SLAB = HEADS // 2
-CHUNK = BANK
+CHUNK = 256
 CHUNKS_PER_SLAB = PIXELS // CHUNK
 CHUNKS = SLABS * CHUNKS_PER_SLAB
 UNIT_WORDS = PASSES * P
 HALF_WORDS = 2
 RUN = 4
-GPSIMD_PIXELS = 192
-VECTOR_PIXELS = CHUNK - GPSIMD_PIXELS
 BN_EPS = 1e-5
 INV_STD = 1.0 / math.sqrt(1.0 + BN_EPS)
 MAX_INV_NORM = 1e12
@@ -51,9 +47,9 @@ def tile_transposedattention_fusion_pa_t_kernel(
         x_stage = ctx.enter_context(tc.tile_pool(name="x_stage", bufs=1))
         x_code_pool = ctx.enter_context(tc.tile_pool(name="x_code_pool", bufs=3))
         unit_pool = ctx.enter_context(tc.tile_pool(name="unit_pool", bufs=3))
-        code_pool = ctx.enter_context(tc.tile_pool(name="code_pool", bufs=4))
+        code_pool = ctx.enter_context(tc.tile_pool(name="code_pool", bufs=7))
         small = ctx.enter_context(tc.tile_pool(name="small", bufs=4))
-        psum_y = ctx.enter_context(tc.psum_pool(name="psum_y", bufs=5))
+        psum_y = ctx.enter_context(tc.psum_pool(name="psum_y", bufs=6))
         psum_turned = ctx.enter_context(tc.psum_pool(name="psum_turned", bufs=1))
         psum_scores = ctx.enter_context(tc.psum_pool(name="psum_scores", bufs=1))
 
@@ -71,8 +67,8 @@ def tile_transposedattention_fusion_pa_t_kernel(
                 in_=(k_w, q_w)[side].rearrange("(h o) c -> o h c", o=P)[:, heads, :],
             )
 
-        def load_x(slab, first_chunk, chunks):
-            cols = slice(first_chunk * CHUNK, (first_chunk + chunks) * CHUNK)
+        def load_x(slab, first, pixels):
+            cols = slice(first, first + pixels)
             source = (x1, x2)[slab % SIDES][slab // SIDES].rearrange("(p j) h w -> p j (h w)", j=PACK)
             nc.sync.dma_start(out=x_rows[slab][:, :, cols], in_=source[:, :, cols])
 
@@ -82,14 +78,14 @@ def tile_transposedattention_fusion_pa_t_kernel(
         nc.vector.memset(one[:], 1.0)
 
         load_weight(0, 0)
-        load_x(0, 0, 1)
+        load_x(0, 0, BANK)
         for v, vec in enumerate((k_b, bnk_w, bnk_b, q_b, bnq_w, bnq_b)):
             nc.sync.dma_start(
                 out=vec_rows[HEADS * v : HEADS * (v + 1), :], in_=vec.rearrange("(h o) -> h o", o=P)
             )
         load_weight(0, 1)
-        load_x(0, 1, 1)
-        load_x(1, 0, CHUNKS_PER_SLAB)
+        load_x(0, BANK, BANK)
+        load_x(1, 0, PIXELS)
         load_weight(1, 0)
         load_weight(1, 1)
         temp_bf16 = const.tile([P, HEADS], BF16, name="temp_bf16")
@@ -97,7 +93,7 @@ def tile_transposedattention_fusion_pa_t_kernel(
             out=temp_bf16[:], in_=temperature.rearrange("h a b -> (h a b)").partition_broadcast(P)
         )
         for slab in range(SIDES, SLABS):
-            load_x(slab, 0, CHUNKS_PER_SLAB)
+            load_x(slab, 0, PIXELS)
 
         warm = const.tile([P, 1], F32, name="warm")
         nc.scalar.activation(out=warm[:], in_=one[:], func=ACT.Abs_reciprocal_sqrt)
@@ -113,10 +109,10 @@ def tile_transposedattention_fusion_pa_t_kernel(
             w_codes[side] = const.tile([P, CHANNELS], U32, name="w_codes%d" % side, align_bytes=64)
             w_scales[side] = const.tile([P, CHANNELS], U8, name="w_scales%d" % side, align_bytes=64)
 
-        def turn_weight(side, pair, copy_out):
+        def turn_weight(side, pair, pool, tag, copy_out):
             words = w_rows[side][:].bitcast(F32).rearrange("o (h p u) -> o h u p", h=HEADS, u=HALF_WORDS)
             grouped_words = w_grouped[side][:].bitcast(F32).rearrange("p (h o u) -> p h o u", h=HEADS, u=HALF_WORDS)
-            turned = psum_turned.tile([P, 2, HALF_WORDS, P], F32, tag="turned%d" % pair, name="w_turned")
+            turned = pool.tile([P, 2, HALF_WORDS, P], F32, tag=tag, name="w_turned")
             for i in range(2):
                 for u in range(HALF_WORDS):
                     nc.tensor.transpose(turned[:, i, u, :], words[:, 2 * pair + i, u, :], ident[:])
@@ -171,47 +167,44 @@ def tile_transposedattention_fusion_pa_t_kernel(
         x_codes = {}
         x_scales = {}
 
-        def x_grouped_tile(chunk):
-            if chunk not in x_grouped:
-                x_grouped[chunk] = x_stage.tile(
-                    [P, CHUNK, PACK], BF16, tag="x_grouped", name="x_grouped", align_bytes=64
-                )
-            return x_grouped[chunk]
+        def stage_x(first, pixels):
+            x_grouped[first] = x_stage.tile([P, pixels, PACK], BF16, tag="x_grouped", name="x_grouped", align_bytes=64)
 
         def regroup_x_gpsimd(chunk):
             if not 0 <= chunk < CHUNKS:
                 return
-            slab, c = divmod(chunk, CHUNKS_PER_SLAB)
+            slab, first = divmod(chunk * CHUNK, PIXELS)
+            stage_x(chunk * CHUNK, CHUNK)
             nc.gpsimd.tensor_scalar(
-                out=x_grouped_tile(chunk)[:, VECTOR_PIXELS:CHUNK, :],
-                in0=x_rows[slab][:, :, c * CHUNK + VECTOR_PIXELS : (c + 1) * CHUNK].rearrange("p j n -> p n j"),
+                out=x_grouped[chunk * CHUNK][:],
+                in0=x_rows[slab][:, :, first : first + CHUNK].rearrange("p j n -> p n j"),
                 scalar1=1.0,
                 scalar2=0.0,
                 op0=ALU.mult,
                 op1=ALU.add,
             )
 
-        def regroup_x_vector(chunk, pixels):
-            if not 0 <= chunk < CHUNKS:
+        def regroup_x_vector(position, pixels):
+            if not 0 <= position < SLABS * PIXELS:
                 return
-            slab, c = divmod(chunk, CHUNKS_PER_SLAB)
+            slab, first = divmod(position, PIXELS)
             nc.vector.tensor_copy(
-                out=x_grouped_tile(chunk)[:, 0:pixels, :].rearrange("p (c i) j -> p c j i", i=RUN),
-                in_=x_rows[slab][:, :, c * CHUNK : c * CHUNK + pixels].rearrange("p j (c i) -> p c j i", i=RUN),
+                out=x_grouped[position][:, 0:pixels, :].rearrange("p (c i) j -> p c j i", i=RUN),
+                in_=x_rows[slab][:, :, first : first + pixels].rearrange("p j (c i) -> p c j i", i=RUN),
             )
 
-        def quantise_x(chunk):
-            if not 0 <= chunk < CHUNKS:
+        def quantise_x(position, pixels):
+            if not 0 <= position < SLABS * PIXELS:
                 return
-            slab, c = divmod(chunk, CHUNKS_PER_SLAB)
-            if c == 0:
+            slab, first = divmod(position, PIXELS)
+            if first == 0:
                 x_codes[slab] = x_code_pool.tile([P, PIXELS], U32, tag="x_codes", name="x_codes", align_bytes=64)
                 x_scales[slab] = x_code_pool.tile([P, PIXELS], U8, tag="x_scales", name="x_scales", align_bytes=64)
-            cols = slice(c * CHUNK, (c + 1) * CHUNK)
+            cols = slice(first, first + pixels)
             nc.vector.quantize_mx(
                 out=x_codes[slab][:, cols].bitcast(FP8X4),
                 scales=x_scales[slab][:, cols],
-                in_=x_grouped[chunk][:].rearrange("p n j -> p (n j)"),
+                in_=x_grouped[position][:].rearrange("p n j -> p (n j)"),
             )
 
         y = {}
@@ -307,116 +300,103 @@ def tile_transposedattention_fusion_pa_t_kernel(
             if not 0 <= unit < UNITS:
                 return
             words = normed[unit][:].bitcast(F32)
+            turned_z[unit] = psum_turned.tile([P, PASSES, HALF_WORDS, P], F32, tag="turned", name="turned_z")
             for g in range(PASSES):
-                turned_z[unit, g] = psum_turned.tile([P, HALF_WORDS, P], F32, tag="turned%d" % g, name="turned_z")
                 for u in range(HALF_WORDS):
                     first = (HALF_WORDS * g + u) * P
-                    nc.tensor.transpose(turned_z[unit, g][:, u, :], words[:, first : first + P], ident[:])
+                    nc.tensor.transpose(turned_z[unit][:, g, u, :], words[:, first : first + P], ident[:])
 
-        def regroup(unit, g):
+        def regroup(unit):
             if not 0 <= unit < UNITS:
                 return
-            pair, i = divmod(unit, 2)
-            if i == 0 and g == 0:
-                z_grouped[pair] = unit_pool.tile(
-                    [P, 2 * UNIT_WORDS * PACK], BF16, tag="z_grouped", name="z_grouped", align_bytes=64
-                )
-            grouped_words = z_grouped[pair][:].bitcast(F32).rearrange(
-                "p (i g o u) -> p i g o u", i=2, g=PASSES, u=HALF_WORDS
+            z_grouped[unit] = unit_pool.tile(
+                [P, UNIT_WORDS * PACK], BF16, tag="z_grouped", name="z_grouped", align_bytes=64
             )
-            turned_words = turned_z[unit, g][:].rearrange("p u o -> p o u")
-            if g == 0:
-                nc.scalar.copy(out=grouped_words[:, i, g, :, :], in_=turned_words)
-            else:
-                nc.vector.tensor_copy(out=grouped_words[:, i, g, :, :], in_=turned_words)
+            grouped_words = z_grouped[unit][:].bitcast(F32).rearrange("p (g o u) -> p g o u", g=PASSES, u=HALF_WORDS)
+            nc.vector.tensor_copy(out=grouped_words, in_=turned_z[unit][:].rearrange("p g u o -> p g o u"))
 
-        def quantise_pair(pair):
-            if not 0 <= pair < PAIRS:
+        def quantise_unit(unit):
+            if not 0 <= unit < UNITS:
                 return
-            z_codes[pair] = code_pool.tile([P, 2 * UNIT_WORDS], U32, tag="z_codes", name="z_codes", align_bytes=64)
-            z_scales[pair] = code_pool.tile([P, 2 * UNIT_WORDS], U8, tag="z_scales", name="z_scales", align_bytes=64)
+            z_codes[unit] = code_pool.tile([P, UNIT_WORDS], U32, tag="z_codes", name="z_codes", align_bytes=64)
+            z_scales[unit] = code_pool.tile([P, UNIT_WORDS], U8, tag="z_scales", name="z_scales", align_bytes=64)
             nc.vector.quantize_mx(
-                out=z_codes[pair][:].bitcast(FP8X4), scales=z_scales[pair][:], in_=z_grouped[pair][:]
+                out=z_codes[unit][:].bitcast(FP8X4), scales=z_scales[unit][:], in_=z_grouped[unit][:]
             )
 
-        def is_q_pair(pair):
-            return 0 <= pair < PAIRS and (pair // PAIRS_PER_SLAB) % SIDES == 1
+        def is_q_unit(unit):
+            return 0 <= unit < UNITS and parts(unit)[1] == 1
 
-        def scores(pair):
-            if not is_q_pair(pair):
+        def scores(unit):
+            if not is_q_unit(unit):
                 return
-            k_pair = pair - PAIRS_PER_SLAB
-            scores_acc[pair] = psum_scores.tile([P, 2, P], F32, tag="scores", name="scores_acc")
-            for i in range(2):
-                for g in range(PASSES):
-                    cols = slice(i * UNIT_WORDS + g * P, i * UNIT_WORDS + (g + 1) * P)
-                    nc.tensor.matmul_mx(
-                        out=scores_acc[pair][:, i, :],
-                        lhsT=z_codes[pair][:, cols].bitcast(FP8X4),
-                        lhsT_scale=z_scales[pair][:, cols],
-                        rhs=z_codes[k_pair][:, cols].bitcast(FP8X4),
-                        rhs_scale=z_scales[k_pair][:, cols],
-                        start=(g == 0),
-                        stop=(g == PASSES - 1),
-                    )
+            k_unit = unit - HEADS
+            scores_acc[unit] = psum_scores.tile([P, P], F32, tag="scores", name="scores_acc")
+            for g in range(PASSES):
+                cols = slice(g * P, (g + 1) * P)
+                nc.tensor.matmul_mx(
+                    out=scores_acc[unit][:],
+                    lhsT=z_codes[unit][:, cols].bitcast(FP8X4),
+                    lhsT_scale=z_scales[unit][:, cols],
+                    rhs=z_codes[k_unit][:, cols].bitcast(FP8X4),
+                    rhs_scale=z_scales[k_unit][:, cols],
+                    start=(g == 0),
+                    stop=(g == PASSES - 1),
+                )
 
-        def store(pair):
-            if not is_q_pair(pair):
+        def store(unit):
+            if not is_q_unit(unit):
                 return
-            batch = pair // (SIDES * PAIRS_PER_SLAB)
-            heads = slice(2 * (pair % PAIRS_PER_SLAB), 2 * (pair % PAIRS_PER_SLAB) + 2)
-            result = small.tile([P, 2, P], F32, tag="result", name="result")
+            slab, side, head = parts(unit)
+            result = small.tile([P, P], F32, tag="result", name="result")
             nc.vector.tensor_tensor(
-                out=result[:], in0=scores_acc[pair][:], in1=temp_full[:, heads, :], op=ALU.mult
+                out=result[:], in0=scores_acc[unit][:], in1=temp_full[:, head, :], op=ALU.mult
             )
-            nc.sync.dma_start(out=out[batch, heads].rearrange("h c d -> c h d"), in_=result[:])
+            nc.sync.dma_start(out=out[slab // SIDES, head], in_=result[:])
 
         def step(s):
-            even = s % 2 == 0
-            normalise(s - 1, 0)
-            project(s + 1, 0)
             turn(s - 2)
-            if not even:
-                scores((s - 5) // 2)
-            project(s + 1, 1)
+            scores(s - 4)
+            normalise(s - 1, 0)
+            project(s + 2, 0)
             sum_squares(s, 0)
             sum_squares(s, 1)
             normalise(s - 1, 1)
+            project(s + 2, 1)
             inverse_norm(s)
-            regroup(s - 2, 0)
-            regroup(s - 2, 1)
-            if even:
-                quantise_pair((s - 4) // 2)
-            else:
-                store((s - 5) // 2)
+            regroup(s - 2)
+            store(s - 4)
+            if s + 6 < FIRST_SHARED_CHUNK:
+                stage_x((s + 6) * CHUNK, CHUNK)
+                regroup_x_vector((s + 6) * CHUNK, CHUNK)
+            quantise_unit(s - 3)
             norm_factors(s)
-            if even:
-                quantise_x((s + 4) // 2)
-                regroup_x_gpsimd((s + 6) // 2)
-            else:
-                regroup_x_vector((s + 5) // 2, VECTOR_PIXELS)
+            quantise_x((s + 6) * CHUNK, CHUNK)
+            if s + 7 >= FIRST_SHARED_CHUNK:
+                regroup_x_gpsimd(s + 7)
 
-        FIRST_STEP = -1
-        FIRST_Q_STEP = HEADS - 1
+        FIRST_STEP = -2
+        FIRST_SHARED_CHUNK = 6
         LAST_STEP = UNITS + 3
 
-        turn_weight(0, 0, nc.scalar.copy)
-        turn_weight(0, 1, nc.scalar.copy)
-        regroup_x_vector(0, CHUNK)
+        turn_weight(0, 0, psum_turned, "turned", nc.scalar.copy)
+        turn_weight(0, 1, psum_scores, "scores", nc.scalar.copy)
+        stage_x(0, BANK)
+        regroup_x_vector(0, BANK)
         quantise_weight(0, 0)
-        quantise_x(0)
-        regroup_x_vector(1, CHUNK)
+        quantise_x(0, BANK)
+        stage_x(BANK, BANK)
+        regroup_x_vector(BANK, BANK)
         channel_numbers()
-        quantise_x(1)
-        regroup_x_gpsimd(2)
+        quantise_x(BANK, BANK)
+        step(-2)
         quantise_weight(0, 1)
-        for s in range(FIRST_STEP, FIRST_Q_STEP - 2):
-            step(s)
-        turn_weight(1, 0, nc.vector.tensor_copy)
-        turn_weight(1, 1, nc.vector.tensor_copy)
-        step(FIRST_Q_STEP - 2)
+        step(-1)
+        turn_weight(1, 0, psum_turned, "turned", nc.vector.tensor_copy)
+        turn_weight(1, 1, psum_scores, "scores", nc.vector.tensor_copy)
+        step(0)
         quantise_weight(1, 0)
         quantise_weight(1, 1)
         spread_temperature()
-        for s in range(FIRST_Q_STEP - 1, LAST_STEP + 1):
+        for s in range(1, LAST_STEP + 1):
             step(s)

@@ -30,6 +30,12 @@ CHUNKS = SLABS * CHUNKS_PER_SLAB
 UNIT_WORDS = PASSES * P
 HALF_WORDS = 2
 RUN = 4
+GP = 160
+RS = (0,)
+RSMOD = 3
+RSEND = 24
+SA = 320
+SB = 320
 BN_EPS = 1e-5
 INV_STD = 1.0 / math.sqrt(1.0 + BN_EPS)
 MAX_INV_NORM = 1e12
@@ -44,7 +50,8 @@ def tile_transposedattention_fusion_pa_t_kernel(
     with ExitStack() as ctx:
         ctx.enter_context(tc.manual_schedule())
         const = ctx.enter_context(tc.tile_pool(name="const", bufs=1))
-        x_stage = ctx.enter_context(tc.tile_pool(name="x_stage", bufs=1))
+        stage_pool = ctx.enter_context(tc.tile_pool(name="stage_pool", bufs=3))
+        head_stage = ctx.enter_context(tc.tile_pool(name="head_stage", bufs=1))
         x_code_pool = ctx.enter_context(tc.tile_pool(name="x_code_pool", bufs=3))
         unit_pool = ctx.enter_context(tc.tile_pool(name="unit_pool", bufs=3))
         code_pool = ctx.enter_context(tc.tile_pool(name="code_pool", bufs=7))
@@ -72,22 +79,29 @@ def tile_transposedattention_fusion_pa_t_kernel(
             source = (x1, x2)[slab % SIDES][slab // SIDES].rearrange("(p j) h w -> p j (h w)", j=PACK)
             nc.sync.dma_start(out=x_rows[slab][:, :, cols], in_=source[:, :, cols])
 
-        vec_rows = const.tile([P, P], BF16, name="vec_rows")
-        nc.vector.memset(vec_rows[:], 0.0)
+        vec_rows = {}
+        for side in range(SIDES):
+            vec_rows[side] = const.tile([P, P], BF16, name="vec_rows%d" % side)
+            nc.vector.memset(vec_rows[side][:], 0.0)
         one = const.tile([P, 1], F32, name="one")
         nc.vector.memset(one[:], 1.0)
 
-        load_weight(0, 0)
+        def load_vectors(side, queue):
+            for v, vec in enumerate(((k_b, bnk_w, bnk_b), (q_b, bnq_w, bnq_b))[side]):
+                queue.dma_start(
+                    out=vec_rows[side][HEADS * v : HEADS * (v + 1), :], in_=vec.rearrange("(h o) -> h o", o=P)
+                )
+
         load_x(0, 0, BANK)
-        for v, vec in enumerate((k_b, bnk_w, bnk_b, q_b, bnq_w, bnq_b)):
-            nc.sync.dma_start(
-                out=vec_rows[HEADS * v : HEADS * (v + 1), :], in_=vec.rearrange("(h o) -> h o", o=P)
-            )
-        load_weight(0, 1)
+        load_weight(0, 0)
         load_x(0, BANK, BANK)
-        load_x(1, 0, PIXELS)
+        load_vectors(0, nc.scalar)
+        load_weight(0, 1)
+        load_x(1, 0, BANK)
+        load_x(1, BANK, BANK)
         load_weight(1, 0)
         load_weight(1, 1)
+        load_vectors(1, nc.sync)
         temp_bf16 = const.tile([P, HEADS], BF16, name="temp_bf16")
         nc.sync.dma_start(
             out=temp_bf16[:], in_=temperature.rearrange("h a b -> (h a b)").partition_broadcast(P)
@@ -100,6 +114,8 @@ def tile_transposedattention_fusion_pa_t_kernel(
 
         ident = const.tile([P, P], F32, name="ident")
         make_identity(nc, ident[:])
+        ident_bf16 = const.tile([P, P], BF16, name="ident_bf16")
+        nc.vector.tensor_copy(out=ident_bf16[:], in_=ident[:])
 
         w_grouped = {}
         w_codes = {}
@@ -109,16 +125,21 @@ def tile_transposedattention_fusion_pa_t_kernel(
             w_codes[side] = const.tile([P, CHANNELS], U32, name="w_codes%d" % side, align_bytes=64)
             w_scales[side] = const.tile([P, CHANNELS], U8, name="w_scales%d" % side, align_bytes=64)
 
-        def turn_weight(side, pair, pool, tag, copy_out):
+        w_turned = {}
+
+        def turn_weight(side, pair, pool, tag):
             words = w_rows[side][:].bitcast(F32).rearrange("o (h p u) -> o h u p", h=HEADS, u=HALF_WORDS)
-            grouped_words = w_grouped[side][:].bitcast(F32).rearrange("p (h o u) -> p h o u", h=HEADS, u=HALF_WORDS)
             turned = pool.tile([P, 2, HALF_WORDS, P], F32, tag=tag, name="w_turned")
             for i in range(2):
                 for u in range(HALF_WORDS):
                     nc.tensor.transpose(turned[:, i, u, :], words[:, 2 * pair + i, u, :], ident[:])
+            w_turned[side, pair] = turned
+
+        def copy_weight(side, pair, copy_out):
+            grouped_words = w_grouped[side][:].bitcast(F32).rearrange("p (h o u) -> p h o u", h=HEADS, u=HALF_WORDS)
             copy_out(
                 out=grouped_words[:, 2 * pair : 2 * pair + 2, :, :],
-                in_=turned[:].rearrange("p i u o -> p i o u"),
+                in_=w_turned[side, pair][:].rearrange("p i u o -> p i o u"),
             )
 
         def quantise_weight(side, pair):
@@ -133,31 +154,31 @@ def tile_transposedattention_fusion_pa_t_kernel(
         affine = const.tile([P, SIDES, HEADS, 2], F32, name="affine")
         temp_full = const.tile([P, HEADS, P], F32, name="temp_full")
 
-        def channel_numbers():
-            vec_rows_f32 = const.tile([P, P], F32, name="vec_rows_f32")
-            nc.gpsimd.tensor_scalar(
-                out=vec_rows_f32[:], in0=vec_rows[:], scalar1=1.0, scalar2=0.0, op0=ALU.mult, op1=ALU.add
-            )
-            vec_turned = psum_scores.tile([P, P], F32, tag="scores", name="vec_turned")
-            nc.tensor.transpose(vec_turned[:], vec_rows_f32[:], ident[:])
-            vec_cols = const.tile([P, SIDES, 3, HEADS], F32, name="vec_cols")
+        vec_cols = {}
+
+        def vector_columns(side):
+            vec_turned = psum_scores.tile([P, P], BF16, tag="scores", name="vec_turned")
+            nc.tensor.transpose(vec_turned[:], vec_rows[side][:], ident_bf16[:])
+            vec_cols[side] = const.tile([P, 3, HEADS], F32, name="vec_cols%d" % side)
             nc.scalar.copy(
-                out=vec_cols[:].rearrange("o s v h -> o (s v h)"), in_=vec_turned[:, 0 : SIDES * 3 * HEADS]
+                out=vec_cols[side][:].rearrange("o v h -> o (v h)"), in_=vec_turned[:, 0 : 3 * HEADS]
             )
-            scaled_bias = const.tile([P, SIDES, HEADS], F32, name="scaled_bias")
+
+        def channel_numbers(side):
+            scaled_bias = const.tile([P, HEADS], F32, name="scaled_bias%d" % side)
             nc.vector.scalar_tensor_tensor(
                 out=scaled_bias[:],
-                in0=vec_cols[:, :, 0, :],
+                in0=vec_cols[side][:, 0, :],
                 scalar=INV_STD,
-                in1=vec_cols[:, :, 1, :],
+                in1=vec_cols[side][:, 1, :],
                 op0=ALU.mult,
                 op1=ALU.mult,
             )
             nc.vector.tensor_scalar(
-                out=affine[:, :, :, 0], in0=vec_cols[:, :, 1, :], scalar1=INV_STD, scalar2=None, op0=ALU.mult
+                out=affine[:, side, :, 0], in0=vec_cols[side][:, 1, :], scalar1=INV_STD, scalar2=None, op0=ALU.mult
             )
             nc.vector.tensor_tensor(
-                out=affine[:, :, :, 1], in0=scaled_bias[:], in1=vec_cols[:, :, 2, :], op=ALU.add
+                out=affine[:, side, :, 1], in0=scaled_bias[:], in1=vec_cols[side][:, 2, :], op=ALU.add
             )
 
         def spread_temperature():
@@ -168,7 +189,10 @@ def tile_transposedattention_fusion_pa_t_kernel(
         x_scales = {}
 
         def stage_x(first, pixels):
-            x_grouped[first] = x_stage.tile([P, pixels, PACK], BF16, tag="x_grouped", name="x_grouped", align_bytes=64)
+            if pixels == CHUNK:
+                x_grouped[first] = stage_pool.tile([P, pixels, PACK], BF16, tag="stage", name="x_grouped", align_bytes=64)
+            else:
+                x_grouped[first] = head_stage.tile([P, pixels, PACK], BF16, tag="head%d" % first, name="x_head", align_bytes=64)
 
         def regroup_x_gpsimd(chunk):
             if not 0 <= chunk < CHUNKS:
@@ -176,21 +200,21 @@ def tile_transposedattention_fusion_pa_t_kernel(
             slab, first = divmod(chunk * CHUNK, PIXELS)
             stage_x(chunk * CHUNK, CHUNK)
             nc.gpsimd.tensor_scalar(
-                out=x_grouped[chunk * CHUNK][:],
-                in0=x_rows[slab][:, :, first : first + CHUNK].rearrange("p j n -> p n j"),
+                out=x_grouped[chunk * CHUNK][:, CHUNK - GP : CHUNK, :],
+                in0=x_rows[slab][:, :, first + CHUNK - GP : first + CHUNK].rearrange("p j n -> p n j"),
                 scalar1=1.0,
                 scalar2=0.0,
                 op0=ALU.mult,
                 op1=ALU.add,
             )
 
-        def regroup_x_vector(position, pixels):
-            if not 0 <= position < SLABS * PIXELS:
+        def regroup_x(copy, position, start, stop):
+            if not 0 <= position < SLABS * PIXELS or stop <= start:
                 return
             slab, first = divmod(position, PIXELS)
-            nc.vector.tensor_copy(
-                out=x_grouped[position][:, 0:pixels, :].rearrange("p (c i) j -> p c j i", i=RUN),
-                in_=x_rows[slab][:, :, first : first + pixels].rearrange("p j (c i) -> p c j i", i=RUN),
+            copy(
+                out=x_grouped[position][:, start:stop, :].rearrange("p (c i) j -> p c j i", i=RUN),
+                in_=x_rows[slab][:, :, first + start : first + stop].rearrange("p j (c i) -> p c j i", i=RUN),
             )
 
         def quantise_x(position, pixels):
@@ -228,7 +252,9 @@ def tile_transposedattention_fusion_pa_t_kernel(
             slab, side, head = parts(unit)
             rows = slice(head * P, (head + 1) * P)
             cols = slice(half * BANK, (half + 1) * BANK)
-            y[unit, half] = psum_y.tile([P, BANK], F32, tag="y", name="y")
+            if half == 0:
+                for h in range(HALVES):
+                    y[unit, h] = psum_y.tile([P, BANK], F32, tag="y", name="y")
             nc.tensor.matmul_mx(
                 out=y[unit, half][:],
                 lhsT=w_codes[side][:, rows].bitcast(FP8X4),
@@ -286,14 +312,16 @@ def tile_transposedattention_fusion_pa_t_kernel(
                 return
             scale = factors[unit][:, 0:1]
             shift = factors[unit][:, 1:2]
+            cols = slice(half * BANK, (half + 1) * BANK)
             if half == 0:
                 normed[unit] = unit_pool.tile([P, PIXELS], BF16, tag="normed", name="normed")
+            if half == 0:
                 nc.vector.tensor_scalar(
-                    out=normed[unit][:, 0:BANK], in0=y[unit, 0][:], scalar1=scale, scalar2=shift, op0=ALU.mult, op1=ALU.add
+                    out=normed[unit][:, cols], in0=y[unit, half][:], scalar1=scale, scalar2=shift, op0=ALU.mult, op1=ALU.add
                 )
             else:
                 nc.scalar.activation(
-                    out=normed[unit][:, BANK:PIXELS], in_=y[unit, 1][:], func=ACT.Identity, scale=scale, bias=shift
+                    out=normed[unit][:, cols], in_=y[unit, half][:], func=ACT.Identity, scale=scale, bias=shift
                 )
 
         def turn(unit):
@@ -306,14 +334,22 @@ def tile_transposedattention_fusion_pa_t_kernel(
                     first = (HALF_WORDS * g + u) * P
                     nc.tensor.transpose(turned_z[unit][:, g, u, :], words[:, first : first + P], ident[:])
 
+        def regroup_by(unit):
+            if unit == UNITS - 1:
+                return "s"
+            return "s" if unit % RSMOD in RS and unit < RSEND else "v"
+
         def regroup(unit):
             if not 0 <= unit < UNITS:
                 return
-            z_grouped[unit] = unit_pool.tile(
-                [P, UNIT_WORDS * PACK], BF16, tag="z_grouped", name="z_grouped", align_bytes=64
+            z_grouped[unit] = stage_pool.tile(
+                [P, UNIT_WORDS * PACK], BF16, tag="stage", name="z_grouped", align_bytes=64
             )
             grouped_words = z_grouped[unit][:].bitcast(F32).rearrange("p (g o u) -> p g o u", g=PASSES, u=HALF_WORDS)
-            nc.vector.tensor_copy(out=grouped_words, in_=turned_z[unit][:].rearrange("p g u o -> p g o u"))
+            if regroup_by(unit) == "s":
+                nc.scalar.copy(out=grouped_words, in_=turned_z[unit][:].rearrange("p g u o -> p g o u"))
+            else:
+                nc.vector.tensor_copy(out=grouped_words, in_=turned_z[unit][:].rearrange("p g u o -> p g o u"))
 
         def quantise_unit(unit):
             if not 0 <= unit < UNITS:
@@ -354,49 +390,103 @@ def tile_transposedattention_fusion_pa_t_kernel(
             )
             nc.sync.dma_start(out=out[slab // SIDES, head], in_=result[:])
 
+        def v_regroup_x(chunk):
+            stage_x(chunk * CHUNK, CHUNK)
+            regroup_x(nc.vector.tensor_copy, chunk * CHUNK, 0, CHUNK)
+
         def step(s):
             turn(s - 2)
             scores(s - 4)
             normalise(s - 1, 0)
-            project(s + 2, 0)
             sum_squares(s, 0)
             sum_squares(s, 1)
             normalise(s - 1, 1)
-            project(s + 2, 1)
             inverse_norm(s)
             regroup(s - 2)
             store(s - 4)
-            if s + 6 < FIRST_SHARED_CHUNK:
-                stage_x((s + 6) * CHUNK, CHUNK)
-                regroup_x_vector((s + 6) * CHUNK, CHUNK)
-            quantise_unit(s - 3)
+            regroup_x(nc.vector.tensor_copy, (s + 5) * CHUNK, 0, CHUNK - GP)
             norm_factors(s)
-            quantise_x((s + 6) * CHUNK, CHUNK)
-            if s + 7 >= FIRST_SHARED_CHUNK:
-                regroup_x_gpsimd(s + 7)
+            quantise_unit(s - 3)
+            quantise_x((s + 5) * CHUNK, CHUNK)
+            regroup_x_gpsimd(s + 6)
+            project(s + 2, 0)
+            project(s + 2, 1)
 
-        FIRST_STEP = -2
-        FIRST_SHARED_CHUNK = 6
-        LAST_STEP = UNITS + 3
+        LAST_STEP = UNITS
 
-        turn_weight(0, 0, psum_turned, "turned", nc.scalar.copy)
-        turn_weight(0, 1, psum_scores, "scores", nc.scalar.copy)
+        vector_columns(0)
+        turn_weight(0, 0, psum_turned, "turned")
+        turn_weight(0, 1, psum_scores, "scores")
         stage_x(0, BANK)
-        regroup_x_vector(0, BANK)
-        quantise_weight(0, 0)
+        regroup_x(nc.scalar.copy, 0, SA, BANK)
+        regroup_x(nc.vector.tensor_copy, 0, 0, SA)
+        channel_numbers(0)
         quantise_x(0, BANK)
         stage_x(BANK, BANK)
-        regroup_x_vector(BANK, BANK)
-        channel_numbers()
+        copy_weight(0, 0, nc.scalar.copy)
+        regroup_x(nc.scalar.copy, BANK, SB, BANK)
+        regroup_x(nc.vector.tensor_copy, BANK, 0, SB)
+        quantise_weight(0, 0)
+        project(0, 0)
+        project(1, 0)
+        copy_weight(0, 1, nc.scalar.copy)
         quantise_x(BANK, BANK)
-        step(-2)
+        project(0, 1)
+        project(1, 1)
+        sum_squares(0, 0)
+        sum_squares(1, 0)
+        sum_squares(0, 1)
+        sum_squares(1, 1)
         quantise_weight(0, 1)
-        step(-1)
-        turn_weight(1, 0, psum_turned, "turned", nc.vector.tensor_copy)
-        turn_weight(1, 1, psum_scores, "scores", nc.vector.tensor_copy)
-        step(0)
+        project(2, 0)
+        project(2, 1)
+        v_regroup_x(4)
+        v_regroup_x(5)
+        quantise_x(4 * CHUNK, CHUNK)
+        quantise_x(5 * CHUNK, CHUNK)
+        v_regroup_x(6)
+        inverse_norm(0)
+        vector_columns(1)
+        inverse_norm(1)
+        norm_factors(0)
+        norm_factors(1)
+        turn_weight(1, 0, psum_turned, "turned")
+        normalise(0, 0)
+        quantise_x(6 * CHUNK, CHUNK)
+        sum_squares(2, 0)
+        normalise(0, 1)
+        project(3, 0)
+        project(3, 1)
+        copy_weight(1, 0, nc.scalar.copy)
+        turn_weight(1, 1, psum_scores, "scores")
+        turn(0)
+        normalise(1, 0)
+        sum_squares(2, 1)
+        normalise(1, 1)
+        inverse_norm(2)
+        copy_weight(1, 1, nc.scalar.copy)
+        stage_x(7 * CHUNK, CHUNK)
+        regroup(0)
+        regroup_x(nc.vector.tensor_copy, 7 * CHUNK, 0, CHUNK)
+        channel_numbers(1)
+        norm_factors(2)
         quantise_weight(1, 0)
+        quantise_x(7 * CHUNK, CHUNK)
+        regroup_x_gpsimd(8)
         quantise_weight(1, 1)
+        project(4, 0)
+        project(4, 1)
         spread_temperature()
-        for s in range(1, LAST_STEP + 1):
+        for s in range(3, LAST_STEP + 1):
             step(s)
+        U = UNITS
+        turn(U - 1)
+        scores(U - 3)
+        regroup(U - 1)
+        store(U - 3)
+        quantise_unit(U - 2)
+        scores(U - 2)
+        quantise_unit(U - 1)
+        store(U - 2)
+        scores(U - 1)
+        store(U - 1)

@@ -30,7 +30,7 @@ CHUNKS = SLABS * CHUNKS_PER_SLAB
 UNIT_WORDS = PASSES * P
 HALF_WORDS = 2
 RUN = 4
-GP = 160
+GP = 176
 RS = (0,)
 RSMOD = 3
 RSEND = 24
@@ -56,6 +56,7 @@ def tile_transposedattention_fusion_pa_t_kernel(
         unit_pool = ctx.enter_context(tc.tile_pool(name="unit_pool", bufs=3))
         code_pool = ctx.enter_context(tc.tile_pool(name="code_pool", bufs=7))
         small = ctx.enter_context(tc.tile_pool(name="small", bufs=4))
+        results = ctx.enter_context(tc.tile_pool(name="results", bufs=UNITS // SIDES))
         psum_y = ctx.enter_context(tc.psum_pool(name="psum_y", bufs=6))
         psum_turned = ctx.enter_context(tc.psum_pool(name="psum_turned", bufs=1))
         psum_scores = ctx.enter_context(tc.psum_pool(name="psum_scores", bufs=1))
@@ -95,7 +96,7 @@ def tile_transposedattention_fusion_pa_t_kernel(
         load_x(0, 0, BANK)
         load_weight(0, 0)
         load_x(0, BANK, BANK)
-        load_vectors(0, nc.scalar)
+        load_vectors(0, nc.sync)
         load_weight(0, 1)
         load_x(1, 0, BANK)
         load_x(1, BANK, BANK)
@@ -324,11 +325,11 @@ def tile_transposedattention_fusion_pa_t_kernel(
                     out=normed[unit][:, cols], in_=y[unit, half][:], func=ACT.Identity, scale=scale, bias=shift
                 )
 
-        def turn(unit):
+        def turn(unit, pool=psum_turned, tag="turned"):
             if not 0 <= unit < UNITS:
                 return
             words = normed[unit][:].bitcast(F32)
-            turned_z[unit] = psum_turned.tile([P, PASSES, HALF_WORDS, P], F32, tag="turned", name="turned_z")
+            turned_z[unit] = pool.tile([P, PASSES, HALF_WORDS, P], F32, tag=tag, name="turned_z")
             for g in range(PASSES):
                 for u in range(HALF_WORDS):
                     first = (HALF_WORDS * g + u) * P
@@ -363,11 +364,11 @@ def tile_transposedattention_fusion_pa_t_kernel(
         def is_q_unit(unit):
             return 0 <= unit < UNITS and parts(unit)[1] == 1
 
-        def scores(unit):
+        def scores(unit, pool=psum_scores, tag="scores"):
             if not is_q_unit(unit):
                 return
             k_unit = unit - HEADS
-            scores_acc[unit] = psum_scores.tile([P, P], F32, tag="scores", name="scores_acc")
+            scores_acc[unit] = pool.tile([P, P], F32, tag=tag, name="scores_acc")
             for g in range(PASSES):
                 cols = slice(g * P, (g + 1) * P)
                 nc.tensor.matmul_mx(
@@ -384,7 +385,7 @@ def tile_transposedattention_fusion_pa_t_kernel(
             if not is_q_unit(unit):
                 return
             slab, side, head = parts(unit)
-            result = small.tile([P, P], F32, tag="result", name="result")
+            result = results.tile([P, P], F32, tag="result", name="result")
             nc.vector.tensor_tensor(
                 out=result[:], in0=scores_acc[unit][:], in1=temp_full[:, head, :], op=ALU.mult
             )
@@ -404,29 +405,29 @@ def tile_transposedattention_fusion_pa_t_kernel(
             inverse_norm(s)
             regroup(s - 2)
             store(s - 4)
-            regroup_x(nc.vector.tensor_copy, (s + 5) * CHUNK, 0, CHUNK - GP)
             norm_factors(s)
+            regroup_x(nc.vector.tensor_copy, (s + 5) * CHUNK, 0, CHUNK - GP + 2 * RUN)
             quantise_unit(s - 3)
             quantise_x((s + 5) * CHUNK, CHUNK)
             regroup_x_gpsimd(s + 6)
-            project(s + 2, 0)
-            project(s + 2, 1)
+            project(s + 1, 0)
+            project(s + 1, 1)
 
-        LAST_STEP = UNITS
+        LAST_STEP = UNITS - 1
 
-        vector_columns(0)
         turn_weight(0, 0, psum_turned, "turned")
-        turn_weight(0, 1, psum_scores, "scores")
         stage_x(0, BANK)
         regroup_x(nc.scalar.copy, 0, SA, BANK)
         regroup_x(nc.vector.tensor_copy, 0, 0, SA)
-        channel_numbers(0)
-        quantise_x(0, BANK)
-        stage_x(BANK, BANK)
         copy_weight(0, 0, nc.scalar.copy)
+        stage_x(BANK, BANK)
         regroup_x(nc.scalar.copy, BANK, SB, BANK)
         regroup_x(nc.vector.tensor_copy, BANK, 0, SB)
+        quantise_x(0, BANK)
+        vector_columns(0)
         quantise_weight(0, 0)
+        channel_numbers(0)
+        turn_weight(0, 1, psum_turned, "turned")
         project(0, 0)
         project(1, 0)
         copy_weight(0, 1, nc.scalar.copy)
@@ -474,19 +475,24 @@ def tile_transposedattention_fusion_pa_t_kernel(
         quantise_x(7 * CHUNK, CHUNK)
         regroup_x_gpsimd(8)
         quantise_weight(1, 1)
-        project(4, 0)
-        project(4, 1)
         spread_temperature()
         for s in range(3, LAST_STEP + 1):
             step(s)
-        U = UNITS
-        turn(U - 1)
-        scores(U - 3)
-        regroup(U - 1)
-        store(U - 3)
-        quantise_unit(U - 2)
-        scores(U - 2)
-        quantise_unit(U - 1)
-        store(U - 2)
-        scores(U - 1)
-        store(U - 1)
+        last = UNITS - 1
+        normalise(last, 0)
+        normalise(last, 1)
+        turn(last - 1)
+        turn(last, psum_y, "y")
+        scores(last - 3)
+        quantise_unit(last - 2)
+        regroup(last - 1)
+        scores(last - 2, psum_y, "y")
+        regroup(last)
+        quantise_unit(last - 1)
+        scores(last - 1, psum_y, "y")
+        store(last - 3)
+        quantise_unit(last)
+        scores(last, psum_y, "y")
+        store(last - 2)
+        store(last - 1)
+        store(last)

@@ -30,10 +30,7 @@ CHUNKS = SLABS * CHUNKS_PER_SLAB
 UNIT_WORDS = PASSES * P
 HALF_WORDS = 2
 RUN = 4
-GP = 176
-RS = (0,)
-RSMOD = 3
-RSEND = 24
+GP = 224
 SA = 320
 SB = 320
 BN_EPS = 1e-5
@@ -153,7 +150,7 @@ def tile_transposedattention_fusion_pa_t_kernel(
             )
 
         affine = const.tile([P, SIDES, HEADS, 2], F32, name="affine")
-        temp_full = const.tile([P, HEADS, P], F32, name="temp_full")
+        temps = const.tile([P, HEADS], F32, name="temps")
 
         vec_cols = {}
 
@@ -183,7 +180,7 @@ def tile_transposedattention_fusion_pa_t_kernel(
             )
 
         def spread_temperature():
-            nc.vector.tensor_copy(out=temp_full[:], in_=temp_bf16[:].unsqueeze(2).to_broadcast([P, HEADS, P]))
+            nc.vector.tensor_copy(out=temps[:], in_=temp_bf16[:])
 
         x_grouped = {}
         x_codes = {}
@@ -338,7 +335,7 @@ def tile_transposedattention_fusion_pa_t_kernel(
         def regroup_by(unit):
             if unit == UNITS - 1:
                 return "s"
-            return "s" if unit % RSMOD in RS and unit < RSEND else "v"
+            return "v"
 
         def regroup(unit):
             if not 0 <= unit < UNITS:
@@ -386,8 +383,8 @@ def tile_transposedattention_fusion_pa_t_kernel(
                 return
             slab, side, head = parts(unit)
             result = results.tile([P, P], F32, tag="result", name="result")
-            nc.vector.tensor_tensor(
-                out=result[:], in0=scores_acc[unit][:], in1=temp_full[:, head, :], op=ALU.mult
+            nc.vector.tensor_scalar(
+                out=result[:], in0=scores_acc[unit][:], scalar1=temps[:, head : head + 1], scalar2=None, op0=ALU.mult
             )
             nc.sync.dma_start(out=out[slab // SIDES, head], in_=result[:])
 
@@ -401,12 +398,12 @@ def tile_transposedattention_fusion_pa_t_kernel(
             normalise(s - 1, 0)
             sum_squares(s, 0)
             sum_squares(s, 1)
+            regroup_x(nc.scalar.copy, (s + 5) * CHUNK, 0, CHUNK - GP)
             normalise(s - 1, 1)
             inverse_norm(s)
             regroup(s - 2)
             store(s - 4)
             norm_factors(s)
-            regroup_x(nc.vector.tensor_copy, (s + 5) * CHUNK, 0, CHUNK - GP + 2 * RUN)
             quantise_unit(s - 3)
             quantise_x((s + 5) * CHUNK, CHUNK)
             regroup_x_gpsimd(s + 6)
@@ -441,26 +438,25 @@ def tile_transposedattention_fusion_pa_t_kernel(
         quantise_weight(0, 1)
         project(2, 0)
         project(2, 1)
-        v_regroup_x(4)
-        v_regroup_x(5)
-        quantise_x(4 * CHUNK, CHUNK)
-        quantise_x(5 * CHUNK, CHUNK)
+        stage_x(PIXELS, BANK)
+        regroup_x(nc.vector.tensor_copy, PIXELS, 0, BANK)
         v_regroup_x(6)
+        quantise_x(PIXELS, BANK)
         inverse_norm(0)
         vector_columns(1)
         inverse_norm(1)
         norm_factors(0)
         norm_factors(1)
-        turn_weight(1, 0, psum_turned, "turned")
+        turn_weight(1, 0, psum_scores, "scores")
         normalise(0, 0)
         quantise_x(6 * CHUNK, CHUNK)
         sum_squares(2, 0)
         normalise(0, 1)
+        turn(0)
         project(3, 0)
         project(3, 1)
         copy_weight(1, 0, nc.scalar.copy)
         turn_weight(1, 1, psum_scores, "scores")
-        turn(0)
         normalise(1, 0)
         sum_squares(2, 1)
         normalise(1, 1)

import math
from contextlib import ExitStack

import concourse.mybir as mybir
from concourse.masks import make_identity

F32 = mybir.dt.float32
BF16 = mybir.dt.bfloat16
U32 = mybir.dt.uint32
U8 = mybir.dt.uint8
FP8X4 = mybir.dt.float8_e4m3fn_x4
ACT = mybir.ActivationFunctionType
ALU = mybir.AluOpType

P = 128
PACK = 4
BATCH = 4
CHANNELS = 512
PIXELS = 1024
HEADS = 4
SIDES = 2
BANK = 512
HALVES = PIXELS // BANK
PASSES = PIXELS // (P * PACK)
SLABS = BATCH * SIDES
UNITS = SLABS * HEADS
CHUNK = 256
CHUNKS_PER_SLAB = PIXELS // CHUNK
CHUNKS = SLABS * CHUNKS_PER_SLAB
UNIT_WORDS = PASSES * P
HALF_WORDS = 2
RUN = 4
GP = 224
SA = 320
SB = 320
BN_EPS = 1e-5
INV_STD = 1.0 / math.sqrt(1.0 + BN_EPS)
MAX_INV_NORM = 1e12

FLOPS = 2 * SLABS * CHANNELS * CHANNELS * PIXELS + 2 * BATCH * HEADS * P * P * PIXELS


def tile_transposedattention_fusion_pa_t_kernel(
    tc, x1, x2, k_w, k_b, q_w, q_b, temperature, bnk_w, bnk_b, bnq_w, bnq_b, out
):
    nc = tc.nc
    with ExitStack() as ctx:
        ctx.enter_context(tc.manual_schedule())
        const = ctx.enter_context(tc.tile_pool(name="const", bufs=1))
        stage_pool = ctx.enter_context(tc.tile_pool(name="stage_pool", bufs=3))
        head_stage = ctx.enter_context(tc.tile_pool(name="head_stage", bufs=1))
        x_code_pool = ctx.enter_context(tc.tile_pool(name="x_code_pool", bufs=3))
        unit_pool = ctx.enter_context(tc.tile_pool(name="unit_pool", bufs=3))
        code_pool = ctx.enter_context(tc.tile_pool(name="code_pool", bufs=7))
        small = ctx.enter_context(tc.tile_pool(name="small", bufs=4))
        results = ctx.enter_context(tc.tile_pool(name="results", bufs=UNITS // SIDES))
        psum_y = ctx.enter_context(tc.psum_pool(name="psum_y", bufs=6))
        psum_turned = ctx.enter_context(tc.psum_pool(name="psum_turned", bufs=1))
        psum_scores = ctx.enter_context(tc.psum_pool(name="psum_scores", bufs=1))

        w_rows = {}
        x_rows = {}
        for side in range(SIDES):
            w_rows[side] = const.tile([P, HEADS * CHANNELS], BF16, name="w_rows%d" % side)
        for slab in range(SLABS):
            x_rows[slab] = const.tile([P, PACK, PIXELS], BF16, name="x_rows%d" % slab)

        def load_weight(side, pair):
            heads = slice(2 * pair, 2 * pair + 2)
            nc.sync.dma_start(
                out=w_rows[side][:].rearrange("o (h c) -> o h c", h=HEADS)[:, heads, :],
                in_=(k_w, q_w)[side].rearrange("(h o) c -> o h c", o=P)[:, heads, :],
            )

        def load_x(slab, first, pixels):
            cols = slice(first, first + pixels)
            source = (x1, x2)[slab % SIDES][slab // SIDES].rearrange("(p j) h w -> p j (h w)", j=PACK)
            nc.sync.dma_start(out=x_rows[slab][:, :, cols], in_=source[:, :, cols])

        vec_rows = {}
        for side in range(SIDES):
            vec_rows[side] = const.tile([P, P], BF16, name="vec_rows%d" % side)
            nc.vector.memset(vec_rows[side][:], 0.0)
        one = const.tile([P, 1], F32, name="one")
        nc.vector.memset(one[:], 1.0)

        def load_vectors(side, queue):
            for v, vec in enumerate(((k_b, bnk_w, bnk_b), (q_b, bnq_w, bnq_b))[side]):
                queue.dma_start(
                    out=vec_rows[side][HEADS * v : HEADS * (v + 1), :], in_=vec.rearrange("(h o) -> h o", o=P)
                )

        load_x(0, 0, BANK)
        load_weight(0, 0)
        load_x(0, BANK, BANK)
        load_vectors(0, nc.sync)
        load_weight(0, 1)
        load_x(1, 0, BANK)
        load_x(1, BANK, BANK)
        load_weight(1, 0)
        load_weight(1, 1)
        load_vectors(1, nc.sync)
        temp_bf16 = const.tile([P, HEADS], BF16, name="temp_bf16")
        nc.sync.dma_start(
            out=temp_bf16[:], in_=temperature.rearrange("h a b -> (h a b)").partition_broadcast(P)
        )
        for slab in range(SIDES, SLABS):
            load_x(slab, 0, PIXELS)

        warm = const.tile([P, 1], F32, name="warm")
        nc.scalar.activation(out=warm[:], in_=one[:], func=ACT.Abs_reciprocal_sqrt)

        ident = const.tile([P, P], F32, name="ident")
        make_identity(nc, ident[:])
        ident_bf16 = const.tile([P, P], BF16, name="ident_bf16")
        nc.vector.tensor_copy(out=ident_bf16[:], in_=ident[:])

        w_grouped = {}
        w_codes = {}
        w_scales = {}
        for side in range(SIDES):
            w_grouped[side] = const.tile([P, HEADS * P * PACK], BF16, name="w_grouped%d" % side, align_bytes=64)
            w_codes[side] = const.tile([P, CHANNELS], U32, name="w_codes%d" % side, align_bytes=64)
            w_scales[side] = const.tile([P, CHANNELS], U8, name="w_scales%d" % side, align_bytes=64)

        w_turned = {}

        def turn_weight(side, pair, pool, tag):
            words = w_rows[side][:].bitcast(F32).rearrange("o (h p u) -> o h u p", h=HEADS, u=HALF_WORDS)
            turned = pool.tile([P, 2, HALF_WORDS, P], F32, tag=tag, name="w_turned")
            for i in range(2):
                for u in range(HALF_WORDS):
                    nc.tensor.transpose(turned[:, i, u, :], words[:, 2 * pair + i, u, :], ident[:])
            w_turned[side, pair] = turned

        def copy_weight(side, pair, copy_out):
            grouped_words = w_grouped[side][:].bitcast(F32).rearrange("p (h o u) -> p h o u", h=HEADS, u=HALF_WORDS)
            copy_out(
                out=grouped_words[:, 2 * pair : 2 * pair + 2, :, :],
                in_=w_turned[side, pair][:].rearrange("p i u o -> p i o u"),
            )

        def quantise_weight(side, pair):
            rows = slice(2 * pair * P, 2 * (pair + 1) * P)
            values = slice(2 * pair * P * PACK, 2 * (pair + 1) * P * PACK)
            nc.vector.quantize_mx(
                out=w_codes[side][:, rows].bitcast(FP8X4),
                scales=w_scales[side][:, rows],
                in_=w_grouped[side][:, values],
            )

        affine = const.tile([P, SIDES, HEADS, 2], F32, name="affine")
        temps = const.tile([P, HEADS], F32, name="temps")

        vec_cols = {}

        def vector_columns(side):
            vec_turned = psum_scores.tile([P, P], BF16, tag="scores", name="vec_turned")
            nc.tensor.transpose(vec_turned[:], vec_rows[side][:], ident_bf16[:])
            vec_cols[side] = const.tile([P, 3, HEADS], F32, name="vec_cols%d" % side)
            nc.scalar.copy(
                out=vec_cols[side][:].rearrange("o v h -> o (v h)"), in_=vec_turned[:, 0 : 3 * HEADS]
            )

        def channel_numbers(side):
            scaled_bias = const.tile([P, HEADS], F32, name="scaled_bias%d" % side)
            nc.vector.scalar_tensor_tensor(
                out=scaled_bias[:],
                in0=vec_cols[side][:, 0, :],
                scalar=INV_STD,
                in1=vec_cols[side][:, 1, :],
                op0=ALU.mult,
                op1=ALU.mult,
            )
            nc.vector.tensor_scalar(
                out=affine[:, side, :, 0], in0=vec_cols[side][:, 1, :], scalar1=INV_STD, scalar2=None, op0=ALU.mult
            )
            nc.vector.tensor_tensor(
                out=affine[:, side, :, 1], in0=scaled_bias[:], in1=vec_cols[side][:, 2, :], op=ALU.add
            )

        def spread_temperature():
            nc.vector.tensor_copy(out=temps[:], in_=temp_bf16[:])

        x_grouped = {}
        x_codes = {}
        x_scales = {}

        def stage_x(first, pixels):
            if pixels == CHUNK:
                x_grouped[first] = stage_pool.tile([P, pixels, PACK], BF16, tag="stage", name="x_grouped", align_bytes=64)
            else:
                x_grouped[first] = head_stage.tile([P, pixels, PACK], BF16, tag="head%d" % first, name="x_head", align_bytes=64)

        def regroup_x_gpsimd(chunk):
            if not 0 <= chunk < CHUNKS:
                return
            slab, first = divmod(chunk * CHUNK, PIXELS)
            stage_x(chunk * CHUNK, CHUNK)
            nc.gpsimd.tensor_scalar(
                out=x_grouped[chunk * CHUNK][:, CHUNK - GP : CHUNK, :],
                in0=x_rows[slab][:, :, first + CHUNK - GP : first + CHUNK].rearrange("p j n -> p n j"),
                scalar1=1.0,
                scalar2=0.0,
                op0=ALU.mult,
                op1=ALU.add,
            )

        def regroup_x(copy, position, start, stop):
            if not 0 <= position < SLABS * PIXELS or stop <= start:
                return
            slab, first = divmod(position, PIXELS)
            copy(
                out=x_grouped[position][:, start:stop, :].rearrange("p (c i) j -> p c j i", i=RUN),
                in_=x_rows[slab][:, :, first + start : first + stop].rearrange("p j (c i) -> p c j i", i=RUN),
            )

        def quantise_x(position, pixels):
            if not 0 <= position < SLABS * PIXELS:
                return
            slab, first = divmod(position, PIXELS)
            if first == 0:
                x_codes[slab] = x_code_pool.tile([P, PIXELS], U32, tag="x_codes", name="x_codes", align_bytes=64)
                x_scales[slab] = x_code_pool.tile([P, PIXELS], U8, tag="x_scales", name="x_scales", align_bytes=64)
            cols = slice(first, first + pixels)
            nc.vector.quantize_mx(
                out=x_codes[slab][:, cols].bitcast(FP8X4),
                scales=x_scales[slab][:, cols],
                in_=x_grouped[position][:].rearrange("p n j -> p (n j)"),
            )

        y = {}
        sumsq = {}
        inv_norm = {}
        factors = {}
        normed = {}
        turned_z = {}
        z_grouped = {}
        z_codes = {}
        z_scales = {}
        scores_acc = {}

        def parts(unit):
            slab, head = divmod(unit, HEADS)
            return slab, slab % SIDES, head

        def project(unit, half):
            if not 0 <= unit < UNITS:
                return
            slab, side, head = parts(unit)
            rows = slice(head * P, (head + 1) * P)
            cols = slice(half * BANK, (half + 1) * BANK)
            if half == 0:
                for h in range(HALVES):
                    y[unit, h] = psum_y.tile([P, BANK], F32, tag="y", name="y")
            nc.tensor.matmul_mx(
                out=y[unit, half][:],
                lhsT=w_codes[side][:, rows].bitcast(FP8X4),
                lhsT_scale=w_scales[side][:, rows],
                rhs=x_codes[slab][:, cols].bitcast(FP8X4),
                rhs_scale=x_scales[slab][:, cols],
                start=True,
                stop=True,
            )

        def sum_squares(unit, half):
            if not 0 <= unit < UNITS:
                return
            slab, side, head = parts(unit)
            if half == 0:
                sumsq[unit] = small.tile([P, HALVES], F32, tag="sumsq", name="sumsq")
            squares = small.tile([P, BANK], BF16, tag="squares", name="squares")
            nc.scalar.activation(
                out=squares[:],
                in_=y[unit, half][:],
                func=ACT.Square,
                scale=affine[:, side, head, 0:1],
                bias=affine[:, side, head, 1:2],
                accum_out=sumsq[unit][:, half : half + 1],
            )

        def inverse_norm(unit):
            if not 0 <= unit < UNITS:
                return
            inv_norm[unit] = small.tile([P, 1], F32, tag="inv_norm", name="inv_norm")
            nc.scalar.activation(
                out=inv_norm[unit][:],
                in_=sumsq[unit][:, 0:1],
                func=ACT.Abs_reciprocal_sqrt,
                bias=sumsq[unit][:, 1:2],
                scale=1.0,
            )

        def norm_factors(unit):
            if not 0 <= unit < UNITS:
                return
            slab, side, head = parts(unit)
            factors[unit] = small.tile([P, 2], F32, tag="factors", name="factors")
            nc.vector.scalar_tensor_tensor(
                out=factors[unit][:],
                in0=inv_norm[unit][:].to_broadcast([P, 2]),
                scalar=MAX_INV_NORM,
                in1=affine[:, side, head, :],
                op0=ALU.min,
                op1=ALU.mult,
            )

        def normalise(unit, half):
            if not 0 <= unit < UNITS:
                return
            scale = factors[unit][:, 0:1]
            shift = factors[unit][:, 1:2]
            cols = slice(half * BANK, (half + 1) * BANK)
            if half == 0:
                normed[unit] = unit_pool.tile([P, PIXELS], BF16, tag="normed", name="normed")
            if half == 0:
                nc.vector.tensor_scalar(
                    out=normed[unit][:, cols], in0=y[unit, half][:], scalar1=scale, scalar2=shift, op0=ALU.mult, op1=ALU.add
                )
            else:
                nc.scalar.activation(
                    out=normed[unit][:, cols], in_=y[unit, half][:], func=ACT.Identity, scale=scale, bias=shift
                )

        def turn(unit, pool=psum_turned, tag="turned"):
            if not 0 <= unit < UNITS:
                return
            words = normed[unit][:].bitcast(F32)
            turned_z[unit] = pool.tile([P, PASSES, HALF_WORDS, P], F32, tag=tag, name="turned_z")
            for g in range(PASSES):
                for u in range(HALF_WORDS):
                    first = (HALF_WORDS * g + u) * P
                    nc.tensor.transpose(turned_z[unit][:, g, u, :], words[:, first : first + P], ident[:])

        def regroup_by(unit):
            if unit == UNITS - 1:
                return "s"
            return "v"

        def regroup(unit):
            if not 0 <= unit < UNITS:
                return
            z_grouped[unit] = stage_pool.tile(
                [P, UNIT_WORDS * PACK], BF16, tag="stage", name="z_grouped", align_bytes=64
            )
            grouped_words = z_grouped[unit][:].bitcast(F32).rearrange("p (g o u) -> p g o u", g=PASSES, u=HALF_WORDS)
            if regroup_by(unit) == "s":
                nc.scalar.copy(out=grouped_words, in_=turned_z[unit][:].rearrange("p g u o -> p g o u"))
            else:
                nc.vector.tensor_copy(out=grouped_words, in_=turned_z[unit][:].rearrange("p g u o -> p g o u"))

        def quantise_unit(unit):
            if not 0 <= unit < UNITS:
                return
            z_codes[unit] = code_pool.tile([P, UNIT_WORDS], U32, tag="z_codes", name="z_codes", align_bytes=64)
            z_scales[unit] = code_pool.tile([P, UNIT_WORDS], U8, tag="z_scales", name="z_scales", align_bytes=64)
            nc.vector.quantize_mx(
                out=z_codes[unit][:].bitcast(FP8X4), scales=z_scales[unit][:], in_=z_grouped[unit][:]
            )

        def is_q_unit(unit):
            return 0 <= unit < UNITS and parts(unit)[1] == 1

        def scores(unit, pool=psum_scores, tag="scores"):
            if not is_q_unit(unit):
                return
            k_unit = unit - HEADS
            scores_acc[unit] = pool.tile([P, P], F32, tag=tag, name="scores_acc")
            for g in range(PASSES):
                cols = slice(g * P, (g + 1) * P)
                nc.tensor.matmul_mx(
                    out=scores_acc[unit][:],
                    lhsT=z_codes[unit][:, cols].bitcast(FP8X4),
                    lhsT_scale=z_scales[unit][:, cols],
                    rhs=z_codes[k_unit][:, cols].bitcast(FP8X4),
                    rhs_scale=z_scales[k_unit][:, cols],
                    start=(g == 0),
                    stop=(g == PASSES - 1),
                )

        def store(unit):
            if not is_q_unit(unit):
                return
            slab, side, head = parts(unit)
            result = results.tile([P, P], F32, tag="result", name="result")
            nc.vector.tensor_scalar(
                out=result[:], in0=scores_acc[unit][:], scalar1=temps[:, head : head + 1], scalar2=None, op0=ALU.mult
            )
            nc.sync.dma_start(out=out[slab // SIDES, head], in_=result[:])

        def v_regroup_x(chunk):
            stage_x(chunk * CHUNK, CHUNK)
            regroup_x(nc.vector.tensor_copy, chunk * CHUNK, 0, CHUNK)

        def step(s):
            turn(s - 2)
            scores(s - 4)
            normalise(s - 1, 0)
            sum_squares(s, 0)
            sum_squares(s, 1)
            regroup_x(nc.scalar.copy, (s + 5) * CHUNK, 0, CHUNK - GP)
            normalise(s - 1, 1)
            inverse_norm(s)
            regroup(s - 2)
            store(s - 4)
            norm_factors(s)
            quantise_unit(s - 3)
            quantise_x((s + 5) * CHUNK, CHUNK)
            regroup_x_gpsimd(s + 6)
            project(s + 1, 0)
            project(s + 1, 1)

        LAST_STEP = UNITS - 1

        turn_weight(0, 0, psum_turned, "turned")
        stage_x(0, BANK)
        regroup_x(nc.scalar.copy, 0, SA, BANK)
        regroup_x(nc.vector.tensor_copy, 0, 0, SA)
        copy_weight(0, 0, nc.scalar.copy)
        stage_x(BANK, BANK)
        regroup_x(nc.scalar.copy, BANK, SB, BANK)
        regroup_x(nc.vector.tensor_copy, BANK, 0, SB)
        quantise_x(0, BANK)
        vector_columns(0)
        quantise_weight(0, 0)
        channel_numbers(0)
        turn_weight(0, 1, psum_turned, "turned")
        project(0, 0)
        project(1, 0)
        copy_weight(0, 1, nc.scalar.copy)
        quantise_x(BANK, BANK)
        project(0, 1)
        project(1, 1)
        sum_squares(0, 0)
        sum_squares(1, 0)
        sum_squares(0, 1)
        sum_squares(1, 1)
        quantise_weight(0, 1)
        project(2, 0)
        project(2, 1)
        stage_x(PIXELS, BANK)
        regroup_x(nc.vector.tensor_copy, PIXELS, 0, BANK)
        v_regroup_x(6)
        quantise_x(PIXELS, BANK)
        inverse_norm(0)
        vector_columns(1)
        inverse_norm(1)
        norm_factors(0)
        norm_factors(1)
        turn_weight(1, 0, psum_scores, "scores")
        normalise(0, 0)
        quantise_x(6 * CHUNK, CHUNK)
        sum_squares(2, 0)
        normalise(0, 1)
        turn(0)
        project(3, 0)
        project(3, 1)
        copy_weight(1, 0, nc.scalar.copy)
        turn_weight(1, 1, psum_scores, "scores")
        normalise(1, 0)
        sum_squares(2, 1)
        normalise(1, 1)
        inverse_norm(2)
        copy_weight(1, 1, nc.scalar.copy)
        stage_x(7 * CHUNK, CHUNK)
        regroup(0)
        regroup_x(nc.vector.tensor_copy, 7 * CHUNK, 0, CHUNK)
        channel_numbers(1)
        norm_factors(2)
        quantise_weight(1, 0)
        quantise_x(7 * CHUNK, CHUNK)
        regroup_x_gpsimd(8)
        quantise_weight(1, 1)
        spread_temperature()
        for s in range(3, LAST_STEP + 1):
            step(s)
        last = UNITS - 1
        normalise(last, 0)
        normalise(last, 1)
        turn(last - 1)
        turn(last, psum_y, "y")
        scores(last - 3)
        quantise_unit(last - 2)
        regroup(last - 1)
        scores(last - 2, psum_y, "y")
        regroup(last)
        quantise_unit(last - 1)
        scores(last - 1, psum_y, "y")
        store(last - 3)
        quantise_unit(last)
        scores(last, psum_y, "y")
        store(last - 2)
        store(last - 1)
        store(last)
